import numpy as np
import ml_dtypes


def mxq(x, axis, fmt="e4m3"):
    dtype, down = {"e4m3": (ml_dtypes.float8_e4m3fn, 7), "e5m2": (ml_dtypes.float8_e5m2, 14)}[fmt]
    v = np.moveaxis(np.asarray(x, np.float32).astype(ml_dtypes.bfloat16).astype(np.float64), axis, -1)
    blocks = v.reshape(v.shape[:-1] + (-1, 32))
    amax = np.abs(blocks).max(-1, keepdims=True)
    byte = np.maximum(np.where(amax > 0, np.frexp(amax)[1] - 1 + 127, 0) - down, 1)
    scale = np.exp2(byte - 127.0)
    codes = (blocks / scale).astype(np.float32).astype(dtype).astype(np.float64)
    return np.moveaxis((codes * scale).reshape(v.shape), -1, axis)


WIDE = False


def mx_kscale(k):
    if not WIDE:
        return np.ones(k)
    levels = np.array([10, -10, 5, -5, 0])
    a = np.random.permutation(np.resize(levels, k // 512 * 4)).reshape(k // 512, 4)
    idx = np.arange(k)
    return np.exp2(a[idx // 512, idx % 128 // 32])


BF16 = ml_dtypes.bfloat16


def bf(x):
    return np.asarray(x, np.float32).astype(BF16)


def f64(x):
    return np.asarray(x).astype(np.float64)


B, D0, D1, D2, D3 = 4096, 1024, 512, 512, 2048
HEBB = 0.01
RATE = 0.001
BATCH_NUM = 1
C = HEBB * RATE / BATCH_NUM


def centred(s):
    return s / np.exp2(np.round(np.log2(s.mean())))


def setup_inputs():
    s, t = centred(mx_kscale(D0)), centred(mx_kscale(D1))
    return {"x": bf((4.0 + 3.0 * np.random.standard_normal((B, D0))) * s),
            "W1": bf(np.random.standard_normal((D1, D0)) * 0.9 / np.sqrt(D0) / s[None, :] * t[:, None]),
            "b1": bf((3.0 + 1.5 * np.random.standard_normal(D1)) * t),
            "W2": bf(np.random.standard_normal((D2, D1)) * 0.9 / np.sqrt(D1) / t[None, :]),
            "b2": bf(3.0 + 1.5 * np.random.standard_normal(D2))}


def reference(x, W1, b1, W2, b2):
    x = f64(x)
    v1 = np.maximum((mxq(x, 1, "e4m3") @ mxq(f64(W1), 1, "e4m3").T) + f64(b1), 0.0)
    m1 = np.mean(v1, axis=0)
    h = v1 + np.sum(x, axis=1, keepdims=True) * (C * m1)[None, :]
    v2 = np.maximum((mxq(h, 1, "e4m3") @ mxq(f64(W2), 1, "e4m3").T) + f64(b2), 0.0)
    m2 = np.mean(v2, axis=0)
    out = v2 + np.sum(h, axis=1, keepdims=True) * (C * m2)[None, :]
    return out, m1, m2

@@ -1,0 +1,349 @@
+from contextlib import ExitStack
+
+import concourse.mybir as mybir
+from concourse.masks import make_identity
+
+F32 = mybir.dt.float32
+BF16 = mybir.dt.bfloat16
+U32 = mybir.dt.uint32
+U8 = mybir.dt.uint8
+FP8X4 = mybir.dt.float8_e4m3fn_x4
+ALU = mybir.AluOpType
+FN = mybir.ActivationFunctionType
+AXIS = mybir.AxisListType
+
+P = 128
+ROWS, D0, D1, D2 = 4096, 1024, 512, 512
+C = 0.01 * 0.001 / 1
+NT = ROWS // P
+CH = 8
+CW = 512
+FLOPS = 2 * ROWS * D0 * D1 + 2 * ROWS * D1 * D2
+
+
+def tile_optimalnet_pa_t_kernel(tc, x, W1, b1, W2, b2, out_0, out_1, out_2):
+    nc = tc.nc
+    x_v = x.rearrange("(p a) i -> p (a i)", a=NT)
+    out_v = out_0.rearrange("(p a) o -> p (a o)", a=NT)
+
+    with ExitStack() as ctx:
+        ctx.enter_context(tc.manual_schedule())
+        keep = ctx.enter_context(tc.tile_pool(name="keep", bufs=1))
+        pt = ctx.enter_context(tc.psum_pool(name="pt", bufs=4))
+        pz = ctx.enter_context(tc.psum_pool(name="pz", bufs=4))
+
+        hv = [keep.tile([P, 4 * CW], F32, name="hv%d" % c) for c in range(CH)]
+        xq = [keep.tile([P, 2 * CW], U32, name="xq%d" % c, align_bytes=64) for c in range(CH)]
+        xs = [keep.tile([P, 2 * CW], U8, name="xs%d" % c, align_bytes=64) for c in range(CH)]
+        w1q = keep.tile([P, 1024], U32, name="w1q", align_bytes=64)
+        w1s = keep.tile([P, 1024], U8, name="w1s", align_bytes=64)
+        w2q = keep.tile([P, 512], U32, name="w2q", align_bytes=64)
+        w2s = keep.tile([P, 512], U8, name="w2s", align_bytes=64)
+        ident = keep.tile([P, P], F32, name="ident")
+        b1f = keep.tile([P, 4], F32, name="b1f")
+        b2f = keep.tile([P, 4], F32, name="b2f")
+        acc1 = keep.tile([P, 32], F32, name="acc1")
+        acc2 = keep.tile([P, 32], F32, name="acc2")
+        sx = keep.tile([P, NT], F32, name="sx")
+        sh = keep.tile([P, NT], F32, name="sh")
+        cm1 = keep.tile([P, 4], F32, name="cm1")
+        s1 = keep.tile([P, 4], F32, name="s1")
+        m1f = keep.tile([P, 4], F32, name="m1f")
+        s2 = keep.tile([P, 4], F32, name="s2")
+        m2f = keep.tile([P, 4], F32, name="m2f")
+        jx = keep.tile([P, D0], BF16, name="jx")
+        ja = keep.tile([P, CW], BF16, name="ja")
+        j8 = keep.tile([P, 8], F32, name="j8")
+        cm2b = keep.tile([P, D2], F32, name="cm2b")
+        m2r = keep.tile([P, D2], F32, name="m2r")
+        m1r = keep.tile([P, D1], F32, name="m1r")
+
+        make_identity(nc, ident[:])
+
+        def four_transposes(bank, words, first):
+            for b in range(4):
+                nc.tensor.transpose(
+                    bank[:, b * P : (b + 1) * P], words[:, first + b * P : first + (b + 1) * P], ident[:]
+                )
+
+        def exit_words(grouped, col0, bank):
+            dst = grouped[:].bitcast(F32).rearrange("q (g c u) -> q g c u", g=2, u=2)
+            nc.scalar.copy(
+                out=dst[:, :, col0 : col0 + P, :],
+                in_=bank[:].rearrange("q (g u c) -> q g c u", g=2, u=2),
+            )
+
+        def layer1(t, c):
+            z = pz.tile([P, CW], F32, name="z", tag="z")
+            for g in range(2):
+                wcols = slice(g * 512 + t * P, g * 512 + (t + 1) * P)
+                xcols = slice(g * CW, (g + 1) * CW)
+                nc.tensor.matmul_mx(
+                    out=z[:],
+                    lhsT=w1q[:, wcols].bitcast(FP8X4),
+                    lhsT_scale=w1s[:, wcols],
+                    rhs=xq[c][:, xcols].bitcast(FP8X4),
+                    rhs_scale=xs[c][:, xcols],
+                    start=(g == 0),
+                    stop=(g == 1),
+                )
+            nc.scalar.activation(
+                out=hv[c][:, t * CW : (t + 1) * CW],
+                in_=z[:],
+                func=FN.Relu,
+                bias=b1f[:, t : t + 1],
+                scale=1.0,
+                accum_out=acc1[:, t * CH + c : t * CH + c + 1],
+            )
+
+        def spread_row_sums(c):
+            sb = pt.tile([P, CW], F32, name="sb", tag="pt")
+            for l in range(4):
+                a = 4 * c + l
+                nc.tensor.transpose(sb[:, l * P : (l + 1) * P], sx[:, a : a + 1].to_broadcast([P, P]), ident[:])
+            return sb
+
+        def scaled_mean1(t):
+            nc.vector.tensor_scalar(
+                out=j8[:],
+                in0=acc1[:, t * CH : (t + 1) * CH],
+                scalar1=C / ROWS,
+                scalar2=None,
+                op0=ALU.mult,
+                op1=ALU.add,
+                accum_out=cm1[:, t : t + 1],
+            )
+
+        def correct(t, c, sb):
+            seg = hv[c][:, t * CW : (t + 1) * CW]
+            nc.vector.scalar_tensor_tensor(
+                out=seg, in0=sb[:], scalar=cm1[:, t : t + 1], in1=seg, op0=ALU.mult, op1=ALU.add
+            )
+
+        with tc.tile_pool(name="stage", bufs=1) as stage:
+            xn = {}
+
+            def load_x(c):
+                xt = stage.tile([P, 4 * D0], BF16, name="xn", tag="xn", bufs=6)
+                nc.sync.dma_start(out=xt[:], in_=x_v[:, c * 4 * D0 : (c + 1) * 4 * D0])
+                xn[c] = xt
+
+            xg = {}
+
+            def transpose_x(c):
+                g_t = stage.tile([P, 4 * D0], BF16, name="xg", tag="xg", bufs=2, align_bytes=64)
+                xg[c] = g_t
+                words = xn[c][:].bitcast(F32)
+                for l in range(4):
+                    bank = pt.tile([P, CW], F32, name="xt", tag="pt")
+                    four_transposes(bank, words, l * 512)
+                    exit_words(g_t, l * P, bank)
+
+            def row_sums_x(c):
+                for l in range(4):
+                    a = 4 * c + l
+                    nc.vector.tensor_scalar(
+                        out=jx[:],
+                        in0=xn[c][:, l * D0 : (l + 1) * D0],
+                        scalar1=1.0,
+                        scalar2=None,
+                        op0=ALU.mult,
+                        op1=ALU.add,
+                        accum_out=sx[:, a : a + 1],
+                    )
+
+            def quantise_x(c):
+                nc.vector.quantize_mx(out=xq[c][:].bitcast(FP8X4), scales=xs[c][:], in_=xg[c][:])
+
+            w1n = stage.tile([P, 4 * D0], BF16, name="w1n")
+            w1g = stage.tile([P, 4 * D0], BF16, name="w1g", align_bytes=64)
+            w2n = stage.tile([P, 4 * D1], BF16, name="w2n")
+            w2g = stage.tile([P, 4 * D1], BF16, name="w2g", align_bytes=64)
+            b1r = stage.tile([P, 4], BF16, name="b1r")
+            b2r = stage.tile([4, P], BF16, name="b2r")
+            b2pad = stage.tile([P, P], F32, name="b2pad")
+
+            load_x(0)
+            nc.sync.dma_start(out=w1n[:], in_=W1.rearrange("(p t) i -> p (t i)", t=4))
+            load_x(1)
+            nc.sync.dma_start(
+                out=w2n[:].rearrange("p (t o) -> p t o", t=4), in_=W2.rearrange("(t p) o -> p t o", p=P)
+            )
+            for c in range(2, 6):
+                load_x(c)
+            nc.scalar.dma_start(out=b1r[:], in_=b1.rearrange("(p t) -> p t", t=4))
+            nc.scalar.dma_start(out=b2r[:], in_=b2.rearrange("(t p) -> t p", p=P))
+
+            nc.vector.memset(b2pad[:], 0.0)
+            nc.vector.tensor_copy(out=b1f[:], in_=b1r[:])
+            nc.vector.tensor_copy(out=b2pad[0:4, :], in_=b2r[:])
+
+            transpose_x(0)
+            row_sums_x(0)
+            w1words = w1n[:].bitcast(F32)
+            for t in range(4):
+                bank = pt.tile([P, CW], F32, name="w1t", tag="pt")
+                four_transposes(bank, w1words, t * 512)
+                exit_words(w1g, t * P, bank)
+            nc.vector.quantize_mx(out=w1q[:].bitcast(FP8X4), scales=w1s[:], in_=w1g[:])
+
+            sbs = {}
+            for c in range(CH):
+                if c + 1 < CH:
+                    transpose_x(c + 1)
+                quantise_x(c)
+                if c + 1 < CH - 1:
+                    row_sums_x(c + 1)
+                if c == CH - 1:
+                    row_sums_x(c)
+                    for cc in range(4):
+                        sbs[cc] = spread_row_sums(cc)
+                layer1(0, c)
+                if c >= 1:
+                    layer1(1, c - 1)
+                if c + 6 < CH:
+                    load_x(c + 6)
+                if c == 2:
+                    w2words = w2n[:].bitcast(F32).rearrange("p (t w u) -> p t u w", t=4, u=2)
+                    w2gw = w2g[:].bitcast(F32).rearrange("q (t c u) -> q t c u", t=4, u=2)
+                    for h in range(2):
+                        bank = pt.tile([P, CW], F32, name="w2t", tag="pt")
+                        for tl in range(2):
+                            for u in range(2):
+                                k = tl * 2 + u
+                                nc.tensor.transpose(
+                                    bank[:, k * P : (k + 1) * P], w2words[:, 2 * h + tl, u, :], ident[:]
+                                )
+                        nc.scalar.copy(
+                            out=w2gw[:, 2 * h : 2 * h + 2, :, :],
+                            in_=bank[:].rearrange("q (t u c) -> q t c u", t=2, u=2),
+                        )
+                    bank = pt.tile([P, CW], F32, name="b2t", tag="pt")
+                    nc.tensor.transpose(bank[:, 0:P], b2pad[:], ident[:])
+                    nc.scalar.copy(out=b2f[:], in_=bank[:, 0:4])
+                if c == 3:
+                    nc.vector.quantize_mx(out=w2q[:].bitcast(FP8X4), scales=w2s[:], in_=w2g[:])
+            layer1(1, CH - 1)
+
+        work = ctx.enter_context(tc.tile_pool(name="work", bufs=1))
+        v2 = [work.tile([P, 4 * CW], F32, name="v2_%d" % c) for c in range(CH)]
+
+        scaled_mean1(0)
+        scaled_mean1(1)
+        for n in range(16):
+            layer1(2 + n // 8, n % 8)
+            if n % 2 == 0:
+                cc = n // 2
+                correct(0, cc, sbs[cc])
+                correct(1, cc, sbs[cc])
+            if n in (6, 8, 10, 12):
+                cc = 4 + (n - 6) // 2
+                sbs[cc] = spread_row_sums(cc)
+        sb2 = {}
+        sb2[0] = spread_row_sums(0)
+        scaled_mean1(2)
+        scaled_mean1(3)
+        for cc in range(1, 4):
+            sb2[cc] = spread_row_sums(cc)
+
+        hg = {}
+
+        def regroup(c):
+            g_t = work.tile([P, 4 * CW], BF16, name="hg", tag="hg", bufs=2, align_bytes=64)
+            hg[c] = g_t
+            nc.vector.tensor_copy(
+                out=g_t[:].rearrange("p (c i t) -> p c t i", i=4, t=4),
+                in_=hv[c][:].rearrange("p (t c i) -> p c t i", t=4, i=4),
+            )
+
+        def layer2(c):
+            hq = work.tile([P, CW], U32, name="hq", tag="hq", bufs=2, align_bytes=64)
+            hs = work.tile([P, CW], U8, name="hs", tag="hs", bufs=2, align_bytes=64)
+            nc.vector.quantize_mx(out=hq[:].bitcast(FP8X4), scales=hs[:], in_=hg[c][:])
+            for t in range(4):
+                z = pz.tile([P, CW], F32, name="z2", tag="z")
+                nc.tensor.matmul_mx(
+                    out=z[:],
+                    lhsT=w2q[:, t * P : (t + 1) * P].bitcast(FP8X4),
+                    lhsT_scale=w2s[:, t * P : (t + 1) * P],
+                    rhs=hq[:].bitcast(FP8X4),
+                    rhs_scale=hs[:],
+                    start=True,
+                    stop=True,
+                )
+                nc.scalar.activation(
+                    out=v2[c][:, t * CW : (t + 1) * CW],
+                    in_=z[:],
+                    func=FN.Relu,
+                    bias=b2f[:, t : t + 1],
+                    scale=1.0,
+                    accum_out=acc2[:, t * CH + c : t * CH + c + 1],
+                )
+
+        for c in range(CH):
+            correct(2, c, sb2[c])
+            correct(3, c, sb2[c])
+            if c + 4 < CH:
+                sb2[c + 4] = spread_row_sums(c + 4)
+            if c >= 1:
+                layer2(c - 1)
+            regroup(c)
+            if c == 0:
+                nc.vector.tensor_reduce(
+                    out=s1[:], in_=acc1[:].rearrange("p (t c) -> p t c", t=4), axis=AXIS.X, op=ALU.add
+                )
+                nc.vector.tensor_scalar_mul(out=m1f[:], in0=s1[:], scalar1=1.0 / ROWS)
+                m1b = pz.tile([P, CW], F32, name="m1b", tag="z")
+                for t in range(4):
+                    nc.tensor.transpose(m1b[:, t * P : (t + 1) * P], m1f[:, t : t + 1].to_broadcast([P, P]), ident[:])
+                nc.scalar.copy(
+                    out=m1r[0:32, :].rearrange("p (k t) -> p k t", t=4),
+                    in_=m1b[0:32, :].rearrange("p (t k) -> p k t", t=4),
+                )
+                nc.sync.dma_start(out=out_1.rearrange("(o n) -> o n", o=1), in_=m1r[0:1, :])
+        layer2(CH - 1)
+
+        def natural(pool, tag, src, l):
+            bank = pool.tile([P, CW], F32, name="nat_" + tag, tag=tag)
+            for t in range(4):
+                nc.tensor.transpose(
+                    bank[:, t * P : (t + 1) * P], src[:, t * CW + l * P : t * CW + (l + 1) * P], ident[:]
+                )
+            return bank
+
+        def row_sum_h(a):
+            bank = natural(pt, "pt", hv[a // 4], a % 4)
+            nc.scalar.activation(out=ja[:], in_=bank[:], func=FN.Copy, accum_out=sh[:, a : a + 1])
+
+        vn = {}
+        for a in range(3):
+            row_sum_h(a)
+        for a in range(4):
+            vn[a] = natural(pz, "z", v2[a // 4], a % 4)
+        nc.vector.tensor_reduce(out=s2[:], in_=acc2[:].rearrange("p (t c) -> p t c", t=4), axis=AXIS.X, op=ALU.add)
+        nc.vector.tensor_scalar_mul(out=m2f[:], in0=s2[:], scalar1=1.0 / ROWS)
+        mb = pt.tile([P, CW], F32, name="mb", tag="pt")
+        for t in range(4):
+            nc.tensor.transpose(mb[:, t * P : (t + 1) * P], m2f[:, t : t + 1].to_broadcast([P, P]), ident[:])
+        nc.scalar.activation(out=cm2b[:], in_=mb[:], func=FN.Copy, scale=C)
+        nc.scalar.copy(out=m2r[0:32, :], in_=mb[0:32, :])
+        nc.sync.dma_start(out=out_2.rearrange("(o n) -> o n", o=1), in_=m2r[0:1, :])
+
+        ob = None
+        for a in range(NT):
+            if a % 2 == 0:
+                ob = work.tile([P, 2 * D2], F32, name="ob", tag="ob", bufs=4)
+            nc.vector.scalar_tensor_tensor(
+                out=ob[:, (a % 2) * D2 : (a % 2 + 1) * D2],
+                in0=cm2b[:],
+                scalar=sh[:, a : a + 1],
+                in1=vn[a][:],
+                op0=ALU.mult,
+                op1=ALU.add,
+            )
+            if a % 2 == 1:
+                nc.sync.dma_start(out=out_v[:, (a - 1) * D2 : (a + 1) * D2], in_=ob[:])
+            if a + 3 < NT:
+                row_sum_h(a + 3)
+            if a + 4 < NT:
+                vn[a + 4] = natural(pz, "z", v2[(a + 4) // 4], (a + 4) % 4)

@@ -32,8 +32,9 @@ def tile_optimalnet_pa_t_kernel(tc, x, W1, b1, W2, b2, out_0, out_1, out_2):
         pt = ctx.enter_context(tc.psum_pool(name="pt", bufs=4))
         pz = ctx.enter_context(tc.psum_pool(name="pz", bufs=4))
 
+        ht = {}
         hv = [keep.tile([P, 4 * CW], F32, name="hv%d" % c) for c in range(CH)]
-        xq = [keep.tile([P, 2 * CW], U32, name="xq%d" % c, align_bytes=64) for c in range(CH)]
+        xq = [keep.tile([P, 2 * CW], U32, name="xq%d" % c, tag="q%d" % c, align_bytes=64) for c in range(CH)]
         xs = [keep.tile([P, 2 * CW], U8, name="xs%d" % c, align_bytes=64) for c in range(CH)]
         w1q = keep.tile([P, 1024], U32, name="w1q", align_bytes=64)
         w1s = keep.tile([P, 1024], U8, name="w1s", align_bytes=64)
@@ -46,6 +47,8 @@ def tile_optimalnet_pa_t_kernel(tc, x, W1, b1, W2, b2, out_0, out_1, out_2):
         acc2 = keep.tile([P, 32], F32, name="acc2")
         sx = keep.tile([P, NT], F32, name="sx")
         sh = keep.tile([P, NT], F32, name="sh")
+        sv = keep.tile([P, NT], F32, name="sv")
+        k1 = keep.tile([P, 1], F32, name="k1")
         cm1 = keep.tile([P, 4], F32, name="cm1")
         s1 = keep.tile([P, 4], F32, name="s1")
         m1f = keep.tile([P, 4], F32, name="m1f")
@@ -115,10 +118,28 @@ def tile_optimalnet_pa_t_kernel(tc, x, W1, b1, W2, b2, out_0, out_1, out_2):
             )
 
         def correct(t, c, sb):
-            seg = hv[c][:, t * CW : (t + 1) * CW]
+            seg = slice(t * CW, (t + 1) * CW)
             nc.vector.scalar_tensor_tensor(
-                out=seg, in0=sb[:], scalar=cm1[:, t : t + 1], in1=seg, op0=ALU.mult, op1=ALU.add
+                out=ht[c][:, seg], in0=sb[:], scalar=cm1[:, t : t + 1], in1=hv[c][:, seg], op0=ALU.mult, op1=ALU.add
             )
+
+        def row_sums_v1(c):
+            bank = pz.tile([P, CW], F32, name="svb", tag="z")
+            for l in range(4):
+                for t in range(4):
+                    nc.tensor.matmul(
+                        out=bank[:, l * P : (l + 1) * P],
+                        lhsT=hv[c][:, t * CW + l * P : t * CW + (l + 1) * P],
+                        rhs=ident[:],
+                        is_transpose=True,
+                        start=(t == 0),
+                        stop=(t == 3),
+                    )
+            for l in range(4):
+                a = 4 * c + l
+                nc.scalar.activation(
+                    out=ja[:, 0:P], in_=bank[:, l * P : (l + 1) * P], func=FN.Copy, accum_out=sv[:, a : a + 1]
+                )
 
         with tc.tile_pool(name="stage", bufs=1) as stage:
             xn = {}
@@ -163,7 +184,10 @@ def tile_optimalnet_pa_t_kernel(tc, x, W1, b1, W2, b2, out_0, out_1, out_2):
             b2r = stage.tile([4, P], BF16, name="b2r")
             b2pad = stage.tile([P, P], F32, name="b2pad")
 
-            load_x(0)
+            first = stage.tile([P, 4 * D0], BF16, name="xn", tag="xn", bufs=6)
+            xn[0] = first
+            for l in range(4):
+                nc.sync.dma_start(out=first[:, l * D0 : (l + 1) * D0], in_=x_v[:, l * D0 : (l + 1) * D0])
             nc.sync.dma_start(out=w1n[:], in_=W1.rearrange("(p t) i -> p (t i)", t=4))
             load_x(1)
             nc.sync.dma_start(
@@ -226,7 +250,9 @@ def tile_optimalnet_pa_t_kernel(tc, x, W1, b1, W2, b2, out_0, out_1, out_2):
             layer1(1, CH - 1)
 
         work = ctx.enter_context(tc.tile_pool(name="work", bufs=1))
-        v2 = [work.tile([P, 4 * CW], F32, name="v2_%d" % c) for c in range(CH)]
+        for c in range(CH):
+            ht[c] = work.tile([P, 4 * CW], BF16, name="ht%d" % c)
+        v2hi = [work.tile([P, 2 * CW], F32, name="v2hi%d" % c) for c in range(CH)]
 
         scaled_mean1(0)
         scaled_mean1(1)
@@ -239,12 +265,26 @@ def tile_optimalnet_pa_t_kernel(tc, x, W1, b1, W2, b2, out_0, out_1, out_2):
             if n in (6, 8, 10, 12):
                 cc = 4 + (n - 6) // 2
                 sbs[cc] = spread_row_sums(cc)
+        v2lo = [keep.tile([P, 2 * CW], F32, name="v2lo%d" % c, tag="q%d" % c, align_bytes=64) for c in range(CH)]
+
+        def v2seg(c, t, first, width):
+            half = v2lo[c] if t < 2 else v2hi[c]
+            return half[:, (t % 2) * CW + first : (t % 2) * CW + first + width]
+
         sb2 = {}
         sb2[0] = spread_row_sums(0)
         scaled_mean1(2)
         scaled_mean1(3)
-        for cc in range(1, 4):
-            sb2[cc] = spread_row_sums(cc)
+        row_sums_v1(0)
+        row_sums_v1(1)
+        sb2[1] = spread_row_sums(1)
+        row_sums_v1(2)
+        sb2[2] = spread_row_sums(2)
+        sb2[3] = spread_row_sums(3)
+        kb = pz.tile([P, CW], F32, name="kb", tag="z")
+        for t in range(4):
+            nc.tensor.transpose(kb[:, t * P : (t + 1) * P], cm1[:, t : t + 1].to_broadcast([P, P]), ident[:])
+        nc.scalar.activation(out=ja[:], in_=kb[:], func=FN.Copy, accum_out=k1[:, 0:1])
 
         hg = {}
 
@@ -253,7 +293,7 @@ def tile_optimalnet_pa_t_kernel(tc, x, W1, b1, W2, b2, out_0, out_1, out_2):
             hg[c] = g_t
             nc.vector.tensor_copy(
                 out=g_t[:].rearrange("p (c i t) -> p c t i", i=4, t=4),
-                in_=hv[c][:].rearrange("p (t c i) -> p c t i", t=4, i=4),
+                in_=ht[c][:].rearrange("p (t c i) -> p c t i", t=4, i=4),
             )
 
         def layer2(c):
@@ -272,7 +312,7 @@ def tile_optimalnet_pa_t_kernel(tc, x, W1, b1, W2, b2, out_0, out_1, out_2):
                     stop=True,
                 )
                 nc.scalar.activation(
-                    out=v2[c][:, t * CW : (t + 1) * CW],
+                    out=v2seg(c, t, 0, CW),
                     in_=z[:],
                     func=FN.Relu,
                     bias=b2f[:, t : t + 1],
@@ -287,6 +327,8 @@ def tile_optimalnet_pa_t_kernel(tc, x, W1, b1, W2, b2, out_0, out_1, out_2):
                 sb2[c + 4] = spread_row_sums(c + 4)
             if c >= 1:
                 layer2(c - 1)
+            if 1 <= c <= 5:
+                row_sums_v1(c + 2)
             regroup(c)
             if c == 0:
                 nc.vector.tensor_reduce(
@@ -303,26 +345,22 @@ def tile_optimalnet_pa_t_kernel(tc, x, W1, b1, W2, b2, out_0, out_1, out_2):
                 nc.sync.dma_start(out=out_1.rearrange("(o n) -> o n", o=1), in_=m1r[0:1, :])
         layer2(CH - 1)
 
-        def natural(pool, tag, src, l):
-            bank = pool.tile([P, CW], F32, name="nat_" + tag, tag=tag)
+        nc.vector.scalar_tensor_tensor(
+            out=sh[:], in0=sx[:], scalar=k1[:, 0:1], in1=sv[:], op0=ALU.mult, op1=ALU.add
+        )
+
+        def natural(a):
+            bank = pt.tile([P, CW], F32, name="vn", tag="pt")
             for t in range(4):
-                nc.tensor.transpose(
-                    bank[:, t * P : (t + 1) * P], src[:, t * CW + l * P : t * CW + (l + 1) * P], ident[:]
-                )
+                nc.tensor.transpose(bank[:, t * P : (t + 1) * P], v2seg(a // 4, t, (a % 4) * P, P), ident[:])
             return bank
 
-        def row_sum_h(a):
-            bank = natural(pt, "pt", hv[a // 4], a % 4)
-            nc.scalar.activation(out=ja[:], in_=bank[:], func=FN.Copy, accum_out=sh[:, a : a + 1])
-
         vn = {}
-        for a in range(3):
-            row_sum_h(a)
         for a in range(4):
-            vn[a] = natural(pz, "z", v2[a // 4], a % 4)
+            vn[a] = natural(a)
         nc.vector.tensor_reduce(out=s2[:], in_=acc2[:].rearrange("p (t c) -> p t c", t=4), axis=AXIS.X, op=ALU.add)
         nc.vector.tensor_scalar_mul(out=m2f[:], in0=s2[:], scalar1=1.0 / ROWS)
-        mb = pt.tile([P, CW], F32, name="mb", tag="pt")
+        mb = pz.tile([P, CW], F32, name="mb", tag="z")
         for t in range(4):
             nc.tensor.transpose(mb[:, t * P : (t + 1) * P], m2f[:, t : t + 1].to_broadcast([P, P]), ident[:])
         nc.scalar.activation(out=cm2b[:], in_=mb[:], func=FN.Copy, scale=C)
@@ -343,7 +381,5 @@ def tile_optimalnet_pa_t_kernel(tc, x, W1, b1, W2, b2, out_0, out_1, out_2):
             )
             if a % 2 == 1:
                 nc.sync.dma_start(out=out_v[:, (a - 1) * D2 : (a + 1) * D2], in_=ob[:])
-            if a + 3 < NT:
-                row_sum_h(a + 3)
             if a + 4 < NT:
-                vn[a + 4] = natural(pz, "z", v2[(a + 4) // 4], (a + 4) % 4)
+                vn[a + 4] = natural(a + 4)

@@ -34,7 +34,8 @@ def tile_optimalnet_pa_t_kernel(tc, x, W1, b1, W2, b2, out_0, out_1, out_2):
 
         ht = {}
         hv = [keep.tile([P, 4 * CW], F32, name="hv%d" % c) for c in range(CH)]
-        xq = [keep.tile([P, 2 * CW], U32, name="xq%d" % c, tag="q%d" % c, align_bytes=64) for c in range(CH)]
+        xq = [keep.tile([P, 2 * CW], U32, name="xq%d" % c, align_bytes=64) for c in range(CH)]
+        sacc = [keep.tile([P, CW], F32, name="sacc%d" % c) for c in range(CH)]
         xs = [keep.tile([P, 2 * CW], U8, name="xs%d" % c, align_bytes=64) for c in range(CH)]
         w1q = keep.tile([P, 1024], U32, name="w1q", align_bytes=64)
         w1s = keep.tile([P, 1024], U8, name="w1s", align_bytes=64)
@@ -51,9 +52,7 @@ def tile_optimalnet_pa_t_kernel(tc, x, W1, b1, W2, b2, out_0, out_1, out_2):
         k1 = keep.tile([P, 1], F32, name="k1")
         cm1 = keep.tile([P, 4], F32, name="cm1")
         s1 = keep.tile([P, 4], F32, name="s1")
-        m1f = keep.tile([P, 4], F32, name="m1f")
         s2 = keep.tile([P, 4], F32, name="s2")
-        m2f = keep.tile([P, 4], F32, name="m2f")
         jx = keep.tile([P, D0], BF16, name="jx")
         ja = keep.tile([P, CW], BF16, name="ja")
         j8 = keep.tile([P, 8], F32, name="j8")
@@ -99,6 +98,12 @@ def tile_optimalnet_pa_t_kernel(tc, x, W1, b1, W2, b2, out_0, out_1, out_2):
                 accum_out=acc1[:, t * CH + c : t * CH + c + 1],
             )
 
+        def add_tiles_01(c):
+            nc.gpsimd.tensor_tensor(out=sacc[c][:], in0=hv[c][:, 0:CW], in1=hv[c][:, CW : 2 * CW], op=ALU.add)
+
+        def add_tile_2(c):
+            nc.gpsimd.tensor_tensor(out=sacc[c][:], in0=sacc[c][:], in1=hv[c][:, 2 * CW : 3 * CW], op=ALU.add)
+
         def spread_row_sums(c):
             sb = pt.tile([P, CW], F32, name="sb", tag="pt")
             for l in range(4):
@@ -126,14 +131,15 @@ def tile_optimalnet_pa_t_kernel(tc, x, W1, b1, W2, b2, out_0, out_1, out_2):
         def row_sums_v1(c):
             bank = pz.tile([P, CW], F32, name="svb", tag="z")
             for l in range(4):
-                for t in range(4):
+                parts = (sacc[c][:, l * P : (l + 1) * P], hv[c][:, 3 * CW + l * P : 3 * CW + (l + 1) * P])
+                for k in range(2):
                     nc.tensor.matmul(
                         out=bank[:, l * P : (l + 1) * P],
-                        lhsT=hv[c][:, t * CW + l * P : t * CW + (l + 1) * P],
+                        lhsT=parts[k],
                         rhs=ident[:],
                         is_transpose=True,
-                        start=(t == 0),
-                        stop=(t == 3),
+                        start=(k == 0),
+                        stop=(k == 1),
                     )
             for l in range(4):
                 a = 4 * c + l
@@ -145,7 +151,7 @@ def tile_optimalnet_pa_t_kernel(tc, x, W1, b1, W2, b2, out_0, out_1, out_2):
             xn = {}
 
             def load_x(c):
-                xt = stage.tile([P, 4 * D0], BF16, name="xn", tag="xn", bufs=6)
+                xt = stage.tile([P, 4 * D0], BF16, name="xn", tag="xn", bufs=5)
                 nc.sync.dma_start(out=xt[:], in_=x_v[:, c * 4 * D0 : (c + 1) * 4 * D0])
                 xn[c] = xt
 
@@ -184,7 +190,7 @@ def tile_optimalnet_pa_t_kernel(tc, x, W1, b1, W2, b2, out_0, out_1, out_2):
             b2r = stage.tile([4, P], BF16, name="b2r")
             b2pad = stage.tile([P, P], F32, name="b2pad")
 
-            first = stage.tile([P, 4 * D0], BF16, name="xn", tag="xn", bufs=6)
+            first = stage.tile([P, 4 * D0], BF16, name="xn", tag="xn", bufs=5)
             xn[0] = first
             for l in range(4):
                 nc.sync.dma_start(out=first[:, l * D0 : (l + 1) * D0], in_=x_v[:, l * D0 : (l + 1) * D0])
@@ -193,7 +199,7 @@ def tile_optimalnet_pa_t_kernel(tc, x, W1, b1, W2, b2, out_0, out_1, out_2):
             nc.sync.dma_start(
                 out=w2n[:].rearrange("p (t o) -> p t o", t=4), in_=W2.rearrange("(t p) o -> p t o", p=P)
             )
-            for c in range(2, 6):
+            for c in range(2, 5):
                 load_x(c)
             nc.scalar.dma_start(out=b1r[:], in_=b1.rearrange("(p t) -> p t", t=4))
             nc.scalar.dma_start(out=b2r[:], in_=b2.rearrange("(t p) -> t p", p=P))
@@ -225,8 +231,9 @@ def tile_optimalnet_pa_t_kernel(tc, x, W1, b1, W2, b2, out_0, out_1, out_2):
                 layer1(0, c)
                 if c >= 1:
                     layer1(1, c - 1)
-                if c + 6 < CH:
-                    load_x(c + 6)
+                    add_tiles_01(c - 1)
+                if c + 5 < CH:
+                    load_x(c + 5)
                 if c == 2:
                     w2words = w2n[:].bitcast(F32).rearrange("p (t w u) -> p t u w", t=4, u=2)
                     w2gw = w2g[:].bitcast(F32).rearrange("q (t c u) -> q t c u", t=4, u=2)
@@ -248,16 +255,19 @@ def tile_optimalnet_pa_t_kernel(tc, x, W1, b1, W2, b2, out_0, out_1, out_2):
                 if c == 3:
                     nc.vector.quantize_mx(out=w2q[:].bitcast(FP8X4), scales=w2s[:], in_=w2g[:])
             layer1(1, CH - 1)
+            add_tiles_01(CH - 1)
 
         work = ctx.enter_context(tc.tile_pool(name="work", bufs=1))
         for c in range(CH):
             ht[c] = work.tile([P, 4 * CW], BF16, name="ht%d" % c)
-        v2hi = [work.tile([P, 2 * CW], F32, name="v2hi%d" % c) for c in range(CH)]
+        v2 = {}
 
         scaled_mean1(0)
         scaled_mean1(1)
         for n in range(16):
             layer1(2 + n // 8, n % 8)
+            if n < 8:
+                add_tile_2(n)
             if n % 2 == 0:
                 cc = n // 2
                 correct(0, cc, sbs[cc])
@@ -265,12 +275,6 @@ def tile_optimalnet_pa_t_kernel(tc, x, W1, b1, W2, b2, out_0, out_1, out_2):
             if n in (6, 8, 10, 12):
                 cc = 4 + (n - 6) // 2
                 sbs[cc] = spread_row_sums(cc)
-        v2lo = [keep.tile([P, 2 * CW], F32, name="v2lo%d" % c, tag="q%d" % c, align_bytes=64) for c in range(CH)]
-
-        def v2seg(c, t, first, width):
-            half = v2lo[c] if t < 2 else v2hi[c]
-            return half[:, (t % 2) * CW + first : (t % 2) * CW + first + width]
-
         sb2 = {}
         sb2[0] = spread_row_sums(0)
         scaled_mean1(2)
@@ -300,6 +304,7 @@ def tile_optimalnet_pa_t_kernel(tc, x, W1, b1, W2, b2, out_0, out_1, out_2):
             hq = work.tile([P, CW], U32, name="hq", tag="hq", bufs=2, align_bytes=64)
             hs = work.tile([P, CW], U8, name="hs", tag="hs", bufs=2, align_bytes=64)
             nc.vector.quantize_mx(out=hq[:].bitcast(FP8X4), scales=hs[:], in_=hg[c][:])
+            v2[c] = keep.tile([P, 4 * CW], F32, name="v2_%d" % c, tag="hv%d" % c)
             for t in range(4):
                 z = pz.tile([P, CW], F32, name="z2", tag="z")
                 nc.tensor.matmul_mx(
@@ -312,7 +317,7 @@ def tile_optimalnet_pa_t_kernel(tc, x, W1, b1, W2, b2, out_0, out_1, out_2):
                     stop=True,
                 )
                 nc.scalar.activation(
-                    out=v2seg(c, t, 0, CW),
+                    out=v2[c][:, t * CW : (t + 1) * CW],
                     in_=z[:],
                     func=FN.Relu,
                     bias=b2f[:, t : t + 1],
@@ -321,26 +326,27 @@ def tile_optimalnet_pa_t_kernel(tc, x, W1, b1, W2, b2, out_0, out_1, out_2):
                 )
 
         for c in range(CH):
+            if 1 <= c <= 5:
+                row_sums_v1(c + 2)
             correct(2, c, sb2[c])
             correct(3, c, sb2[c])
             if c + 4 < CH:
                 sb2[c + 4] = spread_row_sums(c + 4)
             if c >= 1:
                 layer2(c - 1)
-            if 1 <= c <= 5:
-                row_sums_v1(c + 2)
             regroup(c)
             if c == 0:
                 nc.vector.tensor_reduce(
                     out=s1[:], in_=acc1[:].rearrange("p (t c) -> p t c", t=4), axis=AXIS.X, op=ALU.add
                 )
-                nc.vector.tensor_scalar_mul(out=m1f[:], in0=s1[:], scalar1=1.0 / ROWS)
                 m1b = pz.tile([P, CW], F32, name="m1b", tag="z")
                 for t in range(4):
-                    nc.tensor.transpose(m1b[:, t * P : (t + 1) * P], m1f[:, t : t + 1].to_broadcast([P, P]), ident[:])
-                nc.scalar.copy(
+                    nc.tensor.transpose(m1b[:, t * P : (t + 1) * P], s1[:, t : t + 1].to_broadcast([P, P]), ident[:])
+                nc.scalar.activation(
                     out=m1r[0:32, :].rearrange("p (k t) -> p k t", t=4),
                     in_=m1b[0:32, :].rearrange("p (t k) -> p k t", t=4),
+                    func=FN.Copy,
+                    scale=1.0 / ROWS,
                 )
                 nc.sync.dma_start(out=out_1.rearrange("(o n) -> o n", o=1), in_=m1r[0:1, :])
         layer2(CH - 1)
@@ -352,19 +358,19 @@ def tile_optimalnet_pa_t_kernel(tc, x, W1, b1, W2, b2, out_0, out_1, out_2):
         def natural(a):
             bank = pt.tile([P, CW], F32, name="vn", tag="pt")
             for t in range(4):
-                nc.tensor.transpose(bank[:, t * P : (t + 1) * P], v2seg(a // 4, t, (a % 4) * P, P), ident[:])
+                first = t * CW + (a % 4) * P
+                nc.tensor.transpose(bank[:, t * P : (t + 1) * P], v2[a // 4][:, first : first + P], ident[:])
             return bank
 
         vn = {}
         for a in range(4):
             vn[a] = natural(a)
         nc.vector.tensor_reduce(out=s2[:], in_=acc2[:].rearrange("p (t c) -> p t c", t=4), axis=AXIS.X, op=ALU.add)
-        nc.vector.tensor_scalar_mul(out=m2f[:], in0=s2[:], scalar1=1.0 / ROWS)
         mb = pz.tile([P, CW], F32, name="mb", tag="z")
         for t in range(4):
-            nc.tensor.transpose(mb[:, t * P : (t + 1) * P], m2f[:, t : t + 1].to_broadcast([P, P]), ident[:])
-        nc.scalar.activation(out=cm2b[:], in_=mb[:], func=FN.Copy, scale=C)
-        nc.scalar.copy(out=m2r[0:32, :], in_=mb[0:32, :])
+            nc.tensor.transpose(mb[:, t * P : (t + 1) * P], s2[:, t : t + 1].to_broadcast([P, P]), ident[:])
+        nc.scalar.activation(out=cm2b[:], in_=mb[:], func=FN.Copy, scale=C / ROWS)
+        nc.scalar.activation(out=m2r[0:32, :], in_=mb[0:32, :], func=FN.Copy, scale=1.0 / ROWS)
         nc.sync.dma_start(out=out_2.rearrange("(o n) -> o n", o=1), in_=m2r[0:1, :])
 
         ob = None

@@ -47,6 +47,8 @@ def tile_optimalnet_pa_t_kernel(tc, x, W1, b1, W2, b2, out_0, out_1, out_2):
         acc1 = keep.tile([P, 32], F32, name="acc1")
         acc2 = keep.tile([P, 32], F32, name="acc2")
         sx = keep.tile([P, NT], F32, name="sx")
+        sxa = keep.tile([P, CH], F32, name="sxa")
+        jxa = keep.tile([P, D0], BF16, name="jxa")
         sh = keep.tile([P, NT], F32, name="sh")
         sv = keep.tile([P, NT], F32, name="sv")
         k1 = keep.tile([P, 1], F32, name="k1")
@@ -108,7 +110,8 @@ def tile_optimalnet_pa_t_kernel(tc, x, W1, b1, W2, b2, out_0, out_1, out_2):
             sb = pt.tile([P, CW], F32, name="sb", tag="pt")
             for l in range(4):
                 a = 4 * c + l
-                nc.tensor.transpose(sb[:, l * P : (l + 1) * P], sx[:, a : a + 1].to_broadcast([P, P]), ident[:])
+                col = sxa[:, c : c + 1] if l == 3 else sx[:, a : a + 1]
+                nc.tensor.transpose(sb[:, l * P : (l + 1) * P], col.to_broadcast([P, P]), ident[:])
             return sb
 
         def scaled_mean1(t):
@@ -167,7 +170,10 @@ def tile_optimalnet_pa_t_kernel(tc, x, W1, b1, W2, b2, out_0, out_1, out_2):
                     exit_words(g_t, l * P, bank)
 
             def row_sums_x(c):
-                for l in range(4):
+                nc.scalar.activation(
+                    out=jxa[:], in_=xn[c][:, 3 * D0 : 4 * D0], func=FN.Copy, accum_out=sxa[:, c : c + 1]
+                )
+                for l in range(3):
                     a = 4 * c + l
                     nc.vector.tensor_scalar(
                         out=jx[:],
@@ -351,8 +357,14 @@ def tile_optimalnet_pa_t_kernel(tc, x, W1, b1, W2, b2, out_0, out_1, out_2):
                 nc.sync.dma_start(out=out_1.rearrange("(o n) -> o n", o=1), in_=m1r[0:1, :])
         layer2(CH - 1)
 
+        sh_v = sh[:].rearrange("p (c l) -> p c l", l=4)
+        sx_v = sx[:].rearrange("p (c l) -> p c l", l=4)
+        sv_v = sv[:].rearrange("p (c l) -> p c l", l=4)
         nc.vector.scalar_tensor_tensor(
-            out=sh[:], in0=sx[:], scalar=k1[:, 0:1], in1=sv[:], op0=ALU.mult, op1=ALU.add
+            out=sh_v[:, :, 0:3], in0=sx_v[:, :, 0:3], scalar=k1[:, 0:1], in1=sv_v[:, :, 0:3], op0=ALU.mult, op1=ALU.add
+        )
+        nc.vector.scalar_tensor_tensor(
+            out=sh_v[:, :, 3], in0=sxa[:], scalar=k1[:, 0:1], in1=sv_v[:, :, 3], op0=ALU.mult, op1=ALU.add
         )
 
         def natural(a):

@@ -222,24 +222,28 @@ def tile_optimalnet_pa_t_kernel(tc, x, W1, b1, W2, b2, out_0, out_1, out_2):
                 four_transposes(bank, w1words, t * 512)
                 exit_words(w1g, t * P, bank)
             nc.vector.quantize_mx(out=w1q[:].bitcast(FP8X4), scales=w1s[:], in_=w1g[:])
+            transpose_x(1)
+            row_sums_x(1)
+            load_x(5)
+            load_x(6)
 
             sbs = {}
             for c in range(CH):
-                if c + 1 < CH:
-                    transpose_x(c + 1)
                 quantise_x(c)
-                if c + 1 < CH - 1:
-                    row_sums_x(c + 1)
-                if c == CH - 1:
+                if c + 2 < CH - 2:
+                    row_sums_x(c + 2)
+                if c >= CH - 2:
                     row_sums_x(c)
+                layer1(0, c)
+                if c + 2 < CH:
+                    transpose_x(c + 2)
+                if c == CH - 1:
                     for cc in range(4):
                         sbs[cc] = spread_row_sums(cc)
-                layer1(0, c)
-                if c >= 1:
-                    layer1(1, c - 1)
-                    add_tiles_01(c - 1)
-                if c + 5 < CH:
-                    load_x(c + 5)
+                layer1(1, c)
+                add_tiles_01(c)
+                if c == 0:
+                    load_x(7)
                 if c == 2:
                     w2words = w2n[:].bitcast(F32).rearrange("p (t w u) -> p t u w", t=4, u=2)
                     w2gw = w2g[:].bitcast(F32).rearrange("q (t c u) -> q t c u", t=4, u=2)
@@ -260,8 +264,6 @@ def tile_optimalnet_pa_t_kernel(tc, x, W1, b1, W2, b2, out_0, out_1, out_2):
                     nc.scalar.copy(out=b2f[:], in_=bank[:, 0:4])
                 if c == 3:
                     nc.vector.quantize_mx(out=w2q[:].bitcast(FP8X4), scales=w2s[:], in_=w2g[:])
-            layer1(1, CH - 1)
-            add_tiles_01(CH - 1)
 
         work = ctx.enter_context(tc.tile_pool(name="work", bufs=1))
         for c in range(CH):
@@ -306,12 +308,18 @@ def tile_optimalnet_pa_t_kernel(tc, x, W1, b1, W2, b2, out_0, out_1, out_2):
                 in_=ht[c][:].rearrange("p (t c i) -> p c t i", t=4, i=4),
             )
 
-        def layer2(c):
+        hqs = {}
+
+        def quantise_h(c):
             hq = work.tile([P, CW], U32, name="hq", tag="hq", bufs=2, align_bytes=64)
             hs = work.tile([P, CW], U8, name="hs", tag="hs", bufs=2, align_bytes=64)
             nc.vector.quantize_mx(out=hq[:].bitcast(FP8X4), scales=hs[:], in_=hg[c][:])
             v2[c] = keep.tile([P, 4 * CW], F32, name="v2_%d" % c, tag="hv%d" % c)
-            for t in range(4):
+            hqs[c] = (hq, hs)
+
+        def layer2(c, tiles):
+            hq, hs = hqs[c]
+            for t in tiles:
                 z = pz.tile([P, CW], F32, name="z2", tag="z")
                 nc.tensor.matmul_mx(
                     out=z[:],
@@ -332,14 +340,17 @@ def tile_optimalnet_pa_t_kernel(tc, x, W1, b1, W2, b2, out_0, out_1, out_2):
                 )
 
         for c in range(CH):
-            if 1 <= c <= 5:
-                row_sums_v1(c + 2)
             correct(2, c, sb2[c])
             correct(3, c, sb2[c])
+            if c >= 1:
+                quantise_h(c - 1)
+                layer2(c - 1, (0, 1))
+            if 1 <= c <= 5:
+                row_sums_v1(c + 2)
+            if c >= 1:
+                layer2(c - 1, (2, 3))
             if c + 4 < CH:
                 sb2[c + 4] = spread_row_sums(c + 4)
-            if c >= 1:
-                layer2(c - 1)
             regroup(c)
             if c == 0:
                 nc.vector.tensor_reduce(
@@ -355,7 +366,8 @@ def tile_optimalnet_pa_t_kernel(tc, x, W1, b1, W2, b2, out_0, out_1, out_2):
                     scale=1.0 / ROWS,
                 )
                 nc.sync.dma_start(out=out_1.rearrange("(o n) -> o n", o=1), in_=m1r[0:1, :])
-        layer2(CH - 1)
+        quantise_h(CH - 1)
+        layer2(CH - 1, (0, 1, 2, 3))
 
         sh_v = sh[:].rearrange("p (c l) -> p c l", l=4)
         sx_v = sx[:].rearrange("p (c l) -> p c l", l=4)

@@ -33,7 +33,12 @@ def tile_optimalnet_pa_t_kernel(tc, x, W1, b1, W2, b2, out_0, out_1, out_2):
         pz = ctx.enter_context(tc.psum_pool(name="pz", bufs=4))
 
         ht = {}
-        hv = [keep.tile([P, 4 * CW], F32, name="hv%d" % c) for c in range(CH)]
+        hva = [keep.tile([P, 3 * CW], F32, name="hva%d" % c) for c in range(CH)]
+        hvb = [keep.tile([P, CW], F32, name="hvb%d" % c) for c in range(CH)]
+
+        def v1seg(c, t):
+            return hvb[c][:] if t == 3 else hva[c][:, t * CW : (t + 1) * CW]
+
         xq = [keep.tile([P, 2 * CW], U32, name="xq%d" % c, align_bytes=64) for c in range(CH)]
         sacc = [keep.tile([P, CW], F32, name="sacc%d" % c) for c in range(CH)]
         xs = [keep.tile([P, 2 * CW], U8, name="xs%d" % c, align_bytes=64) for c in range(CH)]
@@ -47,10 +52,11 @@ def tile_optimalnet_pa_t_kernel(tc, x, W1, b1, W2, b2, out_0, out_1, out_2):
         acc1 = keep.tile([P, 32], F32, name="acc1")
         acc2 = keep.tile([P, 32], F32, name="acc2")
         sx = keep.tile([P, NT], F32, name="sx")
-        sxa = keep.tile([P, CH], F32, name="sxa")
+        sxa = keep.tile([P, NT], F32, name="sxa")
         jxa = keep.tile([P, D0], BF16, name="jxa")
         sh = keep.tile([P, NT], F32, name="sh")
-        sv = keep.tile([P, NT], F32, name="sv")
+        shb = keep.tile([P, NT], F32, name="shb")
+        shb0 = keep.tile([P, NT], F32, name="shb0")
         k1 = keep.tile([P, 1], F32, name="k1")
         cm1 = keep.tile([P, 4], F32, name="cm1")
         s1 = keep.tile([P, 4], F32, name="s1")
@@ -63,6 +69,8 @@ def tile_optimalnet_pa_t_kernel(tc, x, W1, b1, W2, b2, out_0, out_1, out_2):
         m1r = keep.tile([P, D1], F32, name="m1r")
 
         make_identity(nc, ident[:])
+        nc.vector.memset(sx[:], 0.0)
+        nc.vector.memset(sxa[:], 0.0)
 
         def four_transposes(bank, words, first):
             for b in range(4):
@@ -92,7 +100,7 @@ def tile_optimalnet_pa_t_kernel(tc, x, W1, b1, W2, b2, out_0, out_1, out_2):
                     stop=(g == 1),
                 )
             nc.scalar.activation(
-                out=hv[c][:, t * CW : (t + 1) * CW],
+                out=v1seg(c, t),
                 in_=z[:],
                 func=FN.Relu,
                 bias=b1f[:, t : t + 1],
@@ -101,16 +109,16 @@ def tile_optimalnet_pa_t_kernel(tc, x, W1, b1, W2, b2, out_0, out_1, out_2):
             )
 
         def add_tiles_01(c):
-            nc.gpsimd.tensor_tensor(out=sacc[c][:], in0=hv[c][:, 0:CW], in1=hv[c][:, CW : 2 * CW], op=ALU.add)
+            nc.gpsimd.tensor_tensor(out=sacc[c][:], in0=v1seg(c, 0), in1=v1seg(c, 1), op=ALU.add)
 
         def add_tile_2(c):
-            nc.gpsimd.tensor_tensor(out=sacc[c][:], in0=sacc[c][:], in1=hv[c][:, 2 * CW : 3 * CW], op=ALU.add)
+            nc.gpsimd.tensor_tensor(out=sacc[c][:], in0=sacc[c][:], in1=v1seg(c, 2), op=ALU.add)
 
         def spread_row_sums(c):
             sb = pt.tile([P, CW], F32, name="sb", tag="pt")
             for l in range(4):
                 a = 4 * c + l
-                col = sxa[:, c : c + 1] if l == 3 else sx[:, a : a + 1]
+                col = sxa[:, a : a + 1] if a % 6 == 5 else sx[:, a : a + 1]
                 nc.tensor.transpose(sb[:, l * P : (l + 1) * P], col.to_broadcast([P, P]), ident[:])
             return sb
 
@@ -128,13 +136,13 @@ def tile_optimalnet_pa_t_kernel(tc, x, W1, b1, W2, b2, out_0, out_1, out_2):
         def correct(t, c, sb):
             seg = slice(t * CW, (t + 1) * CW)
             nc.vector.scalar_tensor_tensor(
-                out=ht[c][:, seg], in0=sb[:], scalar=cm1[:, t : t + 1], in1=hv[c][:, seg], op0=ALU.mult, op1=ALU.add
+                out=ht[c][:, seg], in0=sb[:], scalar=cm1[:, t : t + 1], in1=v1seg(c, t), op0=ALU.mult, op1=ALU.add
             )
 
         def row_sums_v1(c):
             bank = pz.tile([P, CW], F32, name="svb", tag="z")
             for l in range(4):
-                parts = (sacc[c][:, l * P : (l + 1) * P], hv[c][:, 3 * CW + l * P : 3 * CW + (l + 1) * P])
+                parts = (sacc[c][:, l * P : (l + 1) * P], hvb[c][:, l * P : (l + 1) * P])
                 for k in range(2):
                     nc.tensor.matmul(
                         out=bank[:, l * P : (l + 1) * P],
@@ -147,7 +155,12 @@ def tile_optimalnet_pa_t_kernel(tc, x, W1, b1, W2, b2, out_0, out_1, out_2):
             for l in range(4):
                 a = 4 * c + l
                 nc.scalar.activation(
-                    out=ja[:, 0:P], in_=bank[:, l * P : (l + 1) * P], func=FN.Copy, accum_out=sv[:, a : a + 1]
+                    out=ja[:, 0:P],
+                    in_=bank[:, l * P : (l + 1) * P],
+                    func=FN.Identity,
+                    bias=shb[:, a : a + 1],
+                    scale=1.0,
+                    accum_out=sh[:, a : a + 1],
                 )
 
         with tc.tile_pool(name="stage", bufs=1) as stage:
@@ -170,20 +183,22 @@ def tile_optimalnet_pa_t_kernel(tc, x, W1, b1, W2, b2, out_0, out_1, out_2):
                     exit_words(g_t, l * P, bank)
 
             def row_sums_x(c):
-                nc.scalar.activation(
-                    out=jxa[:], in_=xn[c][:, 3 * D0 : 4 * D0], func=FN.Copy, accum_out=sxa[:, c : c + 1]
-                )
-                for l in range(3):
+                for l in range(4):
                     a = 4 * c + l
-                    nc.vector.tensor_scalar(
-                        out=jx[:],
-                        in0=xn[c][:, l * D0 : (l + 1) * D0],
-                        scalar1=1.0,
-                        scalar2=None,
-                        op0=ALU.mult,
-                        op1=ALU.add,
-                        accum_out=sx[:, a : a + 1],
-                    )
+                    if a % 6 == 5:
+                        nc.scalar.activation(
+                            out=jxa[:], in_=xn[c][:, l * D0 : (l + 1) * D0], func=FN.Copy, accum_out=sxa[:, a : a + 1]
+                        )
+                    else:
+                        nc.vector.tensor_scalar(
+                            out=jx[:],
+                            in0=xn[c][:, l * D0 : (l + 1) * D0],
+                            scalar1=1.0,
+                            scalar2=None,
+                            op0=ALU.mult,
+                            op1=ALU.add,
+                            accum_out=sx[:, a : a + 1],
+                        )
 
             def quantise_x(c):
                 nc.vector.quantize_mx(out=xq[c][:].bitcast(FP8X4), scales=xs[c][:], in_=xg[c][:])
@@ -287,16 +302,12 @@ def tile_optimalnet_pa_t_kernel(tc, x, W1, b1, W2, b2, out_0, out_1, out_2):
         sb2[0] = spread_row_sums(0)
         scaled_mean1(2)
         scaled_mean1(3)
-        row_sums_v1(0)
-        row_sums_v1(1)
-        sb2[1] = spread_row_sums(1)
-        row_sums_v1(2)
-        sb2[2] = spread_row_sums(2)
-        sb2[3] = spread_row_sums(3)
         kb = pz.tile([P, CW], F32, name="kb", tag="z")
         for t in range(4):
             nc.tensor.transpose(kb[:, t * P : (t + 1) * P], cm1[:, t : t + 1].to_broadcast([P, P]), ident[:])
-        nc.scalar.activation(out=ja[:], in_=kb[:], func=FN.Copy, accum_out=k1[:, 0:1])
+        nc.scalar.activation(out=ja[:], in_=kb[:], func=FN.Copy, scale=1.0 / P, accum_out=k1[:, 0:1])
+        for cc in range(1, 4):
+            sb2[cc] = spread_row_sums(cc)
 
         hg = {}
 
@@ -310,11 +321,19 @@ def tile_optimalnet_pa_t_kernel(tc, x, W1, b1, W2, b2, out_0, out_1, out_2):
 
         hqs = {}
 
+        def v2seg(c, t, first, width):
+            if t == 3:
+                return v2[c][1][:, first : first + width]
+            return v2[c][0][:, t * CW + first : t * CW + first + width]
+
         def quantise_h(c):
             hq = work.tile([P, CW], U32, name="hq", tag="hq", bufs=2, align_bytes=64)
             hs = work.tile([P, CW], U8, name="hs", tag="hs", bufs=2, align_bytes=64)
             nc.vector.quantize_mx(out=hq[:].bitcast(FP8X4), scales=hs[:], in_=hg[c][:])
-            v2[c] = keep.tile([P, 4 * CW], F32, name="v2_%d" % c, tag="hv%d" % c)
+            v2[c] = (
+                keep.tile([P, 3 * CW], F32, name="v2a%d" % c, tag="hva%d" % c),
+                work.tile([P, CW], F32, name="v2b%d" % c),
+            )
             hqs[c] = (hq, hs)
 
         def layer2(c, tiles):
@@ -331,7 +350,7 @@ def tile_optimalnet_pa_t_kernel(tc, x, W1, b1, W2, b2, out_0, out_1, out_2):
                     stop=True,
                 )
                 nc.scalar.activation(
-                    out=v2[c][:, t * CW : (t + 1) * CW],
+                    out=v2seg(c, t, 0, CW),
                     in_=z[:],
                     func=FN.Relu,
                     bias=b2f[:, t : t + 1],
@@ -345,14 +364,18 @@ def tile_optimalnet_pa_t_kernel(tc, x, W1, b1, W2, b2, out_0, out_1, out_2):
             if c >= 1:
                 quantise_h(c - 1)
                 layer2(c - 1, (0, 1))
-            if 1 <= c <= 5:
-                row_sums_v1(c + 2)
             if c >= 1:
                 layer2(c - 1, (2, 3))
             if c + 4 < CH:
                 sb2[c + 4] = spread_row_sums(c + 4)
             regroup(c)
             if c == 0:
+                nc.vector.tensor_scalar_mul(out=shb0[:], in0=sx[:], scalar1=k1[:, 0:1])
+                nc.vector.scalar_tensor_tensor(
+                    out=shb[:], in0=sxa[:], scalar=k1[:, 0:1], in1=shb0[:], op0=ALU.mult, op1=ALU.add
+                )
+                for cc in range(3):
+                    row_sums_v1(cc)
                 nc.vector.tensor_reduce(
                     out=s1[:], in_=acc1[:].rearrange("p (t c) -> p t c", t=4), axis=AXIS.X, op=ALU.add
                 )
@@ -369,21 +392,12 @@ def tile_optimalnet_pa_t_kernel(tc, x, W1, b1, W2, b2, out_0, out_1, out_2):
         quantise_h(CH - 1)
         layer2(CH - 1, (0, 1, 2, 3))
 
-        sh_v = sh[:].rearrange("p (c l) -> p c l", l=4)
-        sx_v = sx[:].rearrange("p (c l) -> p c l", l=4)
-        sv_v = sv[:].rearrange("p (c l) -> p c l", l=4)
-        nc.vector.scalar_tensor_tensor(
-            out=sh_v[:, :, 0:3], in0=sx_v[:, :, 0:3], scalar=k1[:, 0:1], in1=sv_v[:, :, 0:3], op0=ALU.mult, op1=ALU.add
-        )
-        nc.vector.scalar_tensor_tensor(
-            out=sh_v[:, :, 3], in0=sxa[:], scalar=k1[:, 0:1], in1=sv_v[:, :, 3], op0=ALU.mult, op1=ALU.add
-        )
+        row_sums_v1(3)
 
         def natural(a):
             bank = pt.tile([P, CW], F32, name="vn", tag="pt")
             for t in range(4):
-                first = t * CW + (a % 4) * P
-                nc.tensor.transpose(bank[:, t * P : (t + 1) * P], v2[a // 4][:, first : first + P], ident[:])
+                nc.tensor.transpose(bank[:, t * P : (t + 1) * P], v2seg(a // 4, t, (a % 4) * P, P), ident[:])
             return bank
 
         vn = {}
@@ -401,15 +415,20 @@ def tile_optimalnet_pa_t_kernel(tc, x, W1, b1, W2, b2, out_0, out_1, out_2):
         for a in range(NT):
             if a % 2 == 0:
                 ob = work.tile([P, 2 * D2], F32, name="ob", tag="ob", bufs=4)
-            nc.vector.scalar_tensor_tensor(
-                out=ob[:, (a % 2) * D2 : (a % 2 + 1) * D2],
-                in0=cm2b[:],
-                scalar=sh[:, a : a + 1],
-                in1=vn[a][:],
-                op0=ALU.mult,
-                op1=ALU.add,
-            )
+            half = ob[:, (a % 2) * D2 : (a % 2 + 1) * D2]
+            if a % 4 == 2:
+                plain = work.tile([P, D2], F32, name="plain", tag="plain", bufs=2)
+                corr = work.tile([P, D2], F32, name="corr", tag="corr", bufs=2)
+                nc.scalar.copy(out=plain[:], in_=vn[a][:])
+                nc.scalar.activation(out=corr[:], in_=cm2b[:], func=FN.Copy, scale=sh[:, a : a + 1])
+                nc.gpsimd.tensor_tensor(out=half, in0=plain[:], in1=corr[:], op=ALU.add)
+            else:
+                nc.vector.scalar_tensor_tensor(
+                    out=half, in0=cm2b[:], scalar=sh[:, a : a + 1], in1=vn[a][:], op0=ALU.mult, op1=ALU.add
+                )
             if a % 2 == 1:
                 nc.sync.dma_start(out=out_v[:, (a - 1) * D2 : (a + 1) * D2], in_=ob[:])
             if a + 4 < NT:
                 vn[a + 4] = natural(a + 4)
+            if a % 4 == 0 and a // 4 + 4 < CH:
+                row_sums_v1(a // 4 + 4)

@@ -39,8 +39,7 @@ def tile_optimalnet_pa_t_kernel(tc, x, W1, b1, W2, b2, out_0, out_1, out_2):
         def v1seg(c, t):
             return hvb[c][:] if t == 3 else hva[c][:, t * CW : (t + 1) * CW]
 
-        xq = [keep.tile([P, 2 * CW], U32, name="xq%d" % c, align_bytes=64) for c in range(CH)]
-        sacc = [keep.tile([P, CW], F32, name="sacc%d" % c) for c in range(CH)]
+        xq = [keep.tile([P, 2 * CW], U32, name="xq%d" % c, tag="q%d" % c, align_bytes=64) for c in range(CH)]
         xs = [keep.tile([P, 2 * CW], U8, name="xs%d" % c, align_bytes=64) for c in range(CH)]
         w1q = keep.tile([P, 1024], U32, name="w1q", align_bytes=64)
         w1s = keep.tile([P, 1024], U8, name="w1s", align_bytes=64)
@@ -108,12 +107,6 @@ def tile_optimalnet_pa_t_kernel(tc, x, W1, b1, W2, b2, out_0, out_1, out_2):
                 accum_out=acc1[:, t * CH + c : t * CH + c + 1],
             )
 
-        def add_tiles_01(c):
-            nc.gpsimd.tensor_tensor(out=sacc[c][:], in0=v1seg(c, 0), in1=v1seg(c, 1), op=ALU.add)
-
-        def add_tile_2(c):
-            nc.gpsimd.tensor_tensor(out=sacc[c][:], in0=sacc[c][:], in1=v1seg(c, 2), op=ALU.add)
-
         def spread_row_sums(c):
             sb = pt.tile([P, CW], F32, name="sb", tag="pt")
             for l in range(4):
@@ -139,29 +132,20 @@ def tile_optimalnet_pa_t_kernel(tc, x, W1, b1, W2, b2, out_0, out_1, out_2):
                 out=ht[c][:, seg], in0=sb[:], scalar=cm1[:, t : t + 1], in1=v1seg(c, t), op0=ALU.mult, op1=ALU.add
             )
 
-        def row_sums_v1(c):
-            bank = pz.tile([P, CW], F32, name="svb", tag="z")
-            for l in range(4):
-                parts = (sacc[c][:, l * P : (l + 1) * P], hvb[c][:, l * P : (l + 1) * P])
-                for k in range(2):
-                    nc.tensor.matmul(
-                        out=bank[:, l * P : (l + 1) * P],
-                        lhsT=parts[k],
-                        rhs=ident[:],
-                        is_transpose=True,
-                        start=(k == 0),
-                        stop=(k == 1),
-                    )
-            for l in range(4):
-                a = 4 * c + l
-                nc.scalar.activation(
-                    out=ja[:, 0:P],
-                    in_=bank[:, l * P : (l + 1) * P],
-                    func=FN.Identity,
-                    bias=shb[:, a : a + 1],
-                    scale=1.0,
-                    accum_out=sh[:, a : a + 1],
+        def row_sum_h(a):
+            bank = pt.tile([P, CW], F32, name="hn", tag="pt")
+            for t in range(4):
+                nc.tensor.transpose(
+                    bank[:, t * P : (t + 1) * P], v1seg(a // 4, t)[:, (a % 4) * P : (a % 4 + 1) * P], ident[:]
                 )
+            nc.scalar.activation(
+                out=ja[:],
+                in_=bank[:],
+                func=FN.Identity,
+                bias=shb[:, a : a + 1],
+                scale=1.0,
+                accum_out=sh[:, a : a + 1],
+            )
 
         with tc.tile_pool(name="stage", bufs=1) as stage:
             xn = {}
@@ -256,7 +240,6 @@ def tile_optimalnet_pa_t_kernel(tc, x, W1, b1, W2, b2, out_0, out_1, out_2):
                     for cc in range(4):
                         sbs[cc] = spread_row_sums(cc)
                 layer1(1, c)
-                add_tiles_01(c)
                 if c == 0:
                     load_x(7)
                 if c == 2:
@@ -289,8 +272,6 @@ def tile_optimalnet_pa_t_kernel(tc, x, W1, b1, W2, b2, out_0, out_1, out_2):
         scaled_mean1(1)
         for n in range(16):
             layer1(2 + n // 8, n % 8)
-            if n < 8:
-                add_tile_2(n)
             if n % 2 == 0:
                 cc = n // 2
                 correct(0, cc, sbs[cc])
@@ -305,7 +286,7 @@ def tile_optimalnet_pa_t_kernel(tc, x, W1, b1, W2, b2, out_0, out_1, out_2):
         kb = pz.tile([P, CW], F32, name="kb", tag="z")
         for t in range(4):
             nc.tensor.transpose(kb[:, t * P : (t + 1) * P], cm1[:, t : t + 1].to_broadcast([P, P]), ident[:])
-        nc.scalar.activation(out=ja[:], in_=kb[:], func=FN.Copy, scale=1.0 / P, accum_out=k1[:, 0:1])
+        nc.scalar.activation(out=ja[:], in_=kb[:], func=FN.Copy, scale=1.0 / D1, accum_out=k1[:, 0:1])
         for cc in range(1, 4):
             sb2[cc] = spread_row_sums(cc)
 
@@ -322,17 +303,15 @@ def tile_optimalnet_pa_t_kernel(tc, x, W1, b1, W2, b2, out_0, out_1, out_2):
         hqs = {}
 
         def v2seg(c, t, first, width):
-            if t == 3:
-                return v2[c][1][:, first : first + width]
-            return v2[c][0][:, t * CW + first : t * CW + first + width]
+            return v2[c][t // 2][:, (t % 2) * CW + first : (t % 2) * CW + first + width]
 
         def quantise_h(c):
             hq = work.tile([P, CW], U32, name="hq", tag="hq", bufs=2, align_bytes=64)
             hs = work.tile([P, CW], U8, name="hs", tag="hs", bufs=2, align_bytes=64)
             nc.vector.quantize_mx(out=hq[:].bitcast(FP8X4), scales=hs[:], in_=hg[c][:])
             v2[c] = (
-                keep.tile([P, 3 * CW], F32, name="v2a%d" % c, tag="hva%d" % c),
-                work.tile([P, CW], F32, name="v2b%d" % c),
+                keep.tile([P, 2 * CW], F32, name="v2lo%d" % c, tag="q%d" % c, align_bytes=64),
+                work.tile([P, 2 * CW], F32, name="v2hi%d" % c),
             )
             hqs[c] = (hq, hs)
 
@@ -374,8 +353,6 @@ def tile_optimalnet_pa_t_kernel(tc, x, W1, b1, W2, b2, out_0, out_1, out_2):
                 nc.vector.scalar_tensor_tensor(
                     out=shb[:], in0=sxa[:], scalar=k1[:, 0:1], in1=shb0[:], op0=ALU.mult, op1=ALU.add
                 )
-                for cc in range(3):
-                    row_sums_v1(cc)
                 nc.vector.tensor_reduce(
                     out=s1[:], in_=acc1[:].rearrange("p (t c) -> p t c", t=4), axis=AXIS.X, op=ALU.add
                 )
@@ -392,19 +369,19 @@ def tile_optimalnet_pa_t_kernel(tc, x, W1, b1, W2, b2, out_0, out_1, out_2):
         quantise_h(CH - 1)
         layer2(CH - 1, (0, 1, 2, 3))
 
-        row_sums_v1(3)
-
         def natural(a):
-            bank = pt.tile([P, CW], F32, name="vn", tag="pt")
+            bank = pz.tile([P, CW], F32, name="vn", tag="z")
             for t in range(4):
                 nc.tensor.transpose(bank[:, t * P : (t + 1) * P], v2seg(a // 4, t, (a % 4) * P, P), ident[:])
             return bank
 
         vn = {}
+        for a in range(3):
+            row_sum_h(a)
         for a in range(4):
             vn[a] = natural(a)
         nc.vector.tensor_reduce(out=s2[:], in_=acc2[:].rearrange("p (t c) -> p t c", t=4), axis=AXIS.X, op=ALU.add)
-        mb = pz.tile([P, CW], F32, name="mb", tag="z")
+        mb = pt.tile([P, CW], F32, name="mb", tag="pt")
         for t in range(4):
             nc.tensor.transpose(mb[:, t * P : (t + 1) * P], s2[:, t : t + 1].to_broadcast([P, P]), ident[:])
         nc.scalar.activation(out=cm2b[:], in_=mb[:], func=FN.Copy, scale=C / ROWS)
@@ -416,19 +393,12 @@ def tile_optimalnet_pa_t_kernel(tc, x, W1, b1, W2, b2, out_0, out_1, out_2):
             if a % 2 == 0:
                 ob = work.tile([P, 2 * D2], F32, name="ob", tag="ob", bufs=4)
             half = ob[:, (a % 2) * D2 : (a % 2 + 1) * D2]
-            if a % 4 == 2:
-                plain = work.tile([P, D2], F32, name="plain", tag="plain", bufs=2)
-                corr = work.tile([P, D2], F32, name="corr", tag="corr", bufs=2)
-                nc.scalar.copy(out=plain[:], in_=vn[a][:])
-                nc.scalar.activation(out=corr[:], in_=cm2b[:], func=FN.Copy, scale=sh[:, a : a + 1])
-                nc.gpsimd.tensor_tensor(out=half, in0=plain[:], in1=corr[:], op=ALU.add)
-            else:
-                nc.vector.scalar_tensor_tensor(
-                    out=half, in0=cm2b[:], scalar=sh[:, a : a + 1], in1=vn[a][:], op0=ALU.mult, op1=ALU.add
-                )
+            nc.vector.scalar_tensor_tensor(
+                out=half, in0=cm2b[:], scalar=sh[:, a : a + 1], in1=vn[a][:], op0=ALU.mult, op1=ALU.add
+            )
             if a % 2 == 1:
                 nc.sync.dma_start(out=out_v[:, (a - 1) * D2 : (a + 1) * D2], in_=ob[:])
+            if a + 3 < NT:
+                row_sum_h(a + 3)
             if a + 4 < NT:
                 vn[a + 4] = natural(a + 4)
-            if a % 4 == 0 and a // 4 + 4 < CH:
-                row_sums_v1(a // 4 + 4)

@@ -33,13 +33,9 @@ def tile_optimalnet_pa_t_kernel(tc, x, W1, b1, W2, b2, out_0, out_1, out_2):
         pz = ctx.enter_context(tc.psum_pool(name="pz", bufs=4))
 
         ht = {}
-        hva = [keep.tile([P, 3 * CW], F32, name="hva%d" % c) for c in range(CH)]
-        hvb = [keep.tile([P, CW], F32, name="hvb%d" % c) for c in range(CH)]
-
-        def v1seg(c, t):
-            return hvb[c][:] if t == 3 else hva[c][:, t * CW : (t + 1) * CW]
-
-        xq = [keep.tile([P, 2 * CW], U32, name="xq%d" % c, tag="q%d" % c, align_bytes=64) for c in range(CH)]
+        hv = [keep.tile([P, 4 * CW], F32, name="hv%d" % c) for c in range(CH)]
+        xq = [keep.tile([P, 2 * CW], U32, name="xq%d" % c, align_bytes=64) for c in range(CH)]
+        sacc = [keep.tile([P, CW], F32, name="sacc%d" % c) for c in range(CH)]
         xs = [keep.tile([P, 2 * CW], U8, name="xs%d" % c, align_bytes=64) for c in range(CH)]
         w1q = keep.tile([P, 1024], U32, name="w1q", align_bytes=64)
         w1s = keep.tile([P, 1024], U8, name="w1s", align_bytes=64)
@@ -51,11 +47,10 @@ def tile_optimalnet_pa_t_kernel(tc, x, W1, b1, W2, b2, out_0, out_1, out_2):
         acc1 = keep.tile([P, 32], F32, name="acc1")
         acc2 = keep.tile([P, 32], F32, name="acc2")
         sx = keep.tile([P, NT], F32, name="sx")
-        sxa = keep.tile([P, NT], F32, name="sxa")
+        sxa = keep.tile([P, CH], F32, name="sxa")
         jxa = keep.tile([P, D0], BF16, name="jxa")
         sh = keep.tile([P, NT], F32, name="sh")
-        shb = keep.tile([P, NT], F32, name="shb")
-        shb0 = keep.tile([P, NT], F32, name="shb0")
+        sv = keep.tile([P, NT], F32, name="sv")
         k1 = keep.tile([P, 1], F32, name="k1")
         cm1 = keep.tile([P, 4], F32, name="cm1")
         s1 = keep.tile([P, 4], F32, name="s1")
@@ -68,8 +63,6 @@ def tile_optimalnet_pa_t_kernel(tc, x, W1, b1, W2, b2, out_0, out_1, out_2):
         m1r = keep.tile([P, D1], F32, name="m1r")
 
         make_identity(nc, ident[:])
-        nc.vector.memset(sx[:], 0.0)
-        nc.vector.memset(sxa[:], 0.0)
 
         def four_transposes(bank, words, first):
             for b in range(4):
@@ -99,7 +92,7 @@ def tile_optimalnet_pa_t_kernel(tc, x, W1, b1, W2, b2, out_0, out_1, out_2):
                     stop=(g == 1),
                 )
             nc.scalar.activation(
-                out=v1seg(c, t),
+                out=hv[c][:, t * CW : (t + 1) * CW],
                 in_=z[:],
                 func=FN.Relu,
                 bias=b1f[:, t : t + 1],
@@ -107,11 +100,17 @@ def tile_optimalnet_pa_t_kernel(tc, x, W1, b1, W2, b2, out_0, out_1, out_2):
                 accum_out=acc1[:, t * CH + c : t * CH + c + 1],
             )
 
+        def add_tiles_01(c):
+            nc.gpsimd.tensor_tensor(out=sacc[c][:], in0=hv[c][:, 0:CW], in1=hv[c][:, CW : 2 * CW], op=ALU.add)
+
+        def add_tile_2(c):
+            nc.gpsimd.tensor_tensor(out=sacc[c][:], in0=sacc[c][:], in1=hv[c][:, 2 * CW : 3 * CW], op=ALU.add)
+
         def spread_row_sums(c):
             sb = pt.tile([P, CW], F32, name="sb", tag="pt")
             for l in range(4):
                 a = 4 * c + l
-                col = sxa[:, a : a + 1] if a % 6 == 5 else sx[:, a : a + 1]
+                col = sxa[:, c : c + 1] if l == 3 else sx[:, a : a + 1]
                 nc.tensor.transpose(sb[:, l * P : (l + 1) * P], col.to_broadcast([P, P]), ident[:])
             return sb
 
@@ -129,22 +128,33 @@ def tile_optimalnet_pa_t_kernel(tc, x, W1, b1, W2, b2, out_0, out_1, out_2):
         def correct(t, c, sb):
             seg = slice(t * CW, (t + 1) * CW)
             nc.vector.scalar_tensor_tensor(
-                out=ht[c][:, seg], in0=sb[:], scalar=cm1[:, t : t + 1], in1=v1seg(c, t), op0=ALU.mult, op1=ALU.add
+                out=ht[c][:, seg], in0=sb[:], scalar=cm1[:, t : t + 1], in1=hv[c][:, seg], op0=ALU.mult, op1=ALU.add
             )
 
-        def row_sum_h(a):
-            bank = pt.tile([P, CW], F32, name="hn", tag="pt")
-            for t in range(4):
-                nc.tensor.transpose(
-                    bank[:, t * P : (t + 1) * P], v1seg(a // 4, t)[:, (a % 4) * P : (a % 4 + 1) * P], ident[:]
-                )
-            nc.scalar.activation(
-                out=ja[:],
-                in_=bank[:],
-                func=FN.Identity,
-                bias=shb[:, a : a + 1],
-                scale=1.0,
-                accum_out=sh[:, a : a + 1],
+        def row_sums_v1(c, on_scalar):
+            bank = pz.tile([P, CW], F32, name="svb", tag="z")
+            for l in range(4):
+                parts = (sacc[c][:, l * P : (l + 1) * P], hv[c][:, 3 * CW + l * P : 3 * CW + (l + 1) * P])
+                for k in range(2):
+                    nc.tensor.matmul(
+                        out=bank[:, l * P : (l + 1) * P],
+                        lhsT=parts[k],
+                        rhs=ident[:],
+                        is_transpose=True,
+                        start=(k == 0),
+                        stop=(k == 1),
+                    )
+            if on_scalar:
+                for l in range(4):
+                    a = 4 * c + l
+                    nc.scalar.activation(
+                        out=ja[:, 0:P], in_=bank[:, l * P : (l + 1) * P], func=FN.Copy, accum_out=sv[:, a : a + 1]
+                    )
+            return bank
+
+        def reduce_row_sums(c, bank):
+            nc.vector.tensor_reduce(
+                out=sv[:, 4 * c : 4 * c + 4], in_=bank[:].rearrange("p (l k) -> p l k", l=4), axis=AXIS.X, op=ALU.add
             )
 
         with tc.tile_pool(name="stage", bufs=1) as stage:
@@ -167,22 +177,20 @@ def tile_optimalnet_pa_t_kernel(tc, x, W1, b1, W2, b2, out_0, out_1, out_2):
                     exit_words(g_t, l * P, bank)
 
             def row_sums_x(c):
-                for l in range(4):
+                nc.scalar.activation(
+                    out=jxa[:], in_=xn[c][:, 3 * D0 : 4 * D0], func=FN.Copy, accum_out=sxa[:, c : c + 1]
+                )
+                for l in range(3):
                     a = 4 * c + l
-                    if a % 6 == 5:
-                        nc.scalar.activation(
-                            out=jxa[:], in_=xn[c][:, l * D0 : (l + 1) * D0], func=FN.Copy, accum_out=sxa[:, a : a + 1]
-                        )
-                    else:
-                        nc.vector.tensor_scalar(
-                            out=jx[:],
-                            in0=xn[c][:, l * D0 : (l + 1) * D0],
-                            scalar1=1.0,
-                            scalar2=None,
-                            op0=ALU.mult,
-                            op1=ALU.add,
-                            accum_out=sx[:, a : a + 1],
-                        )
+                    nc.vector.tensor_scalar(
+                        out=jx[:],
+                        in0=xn[c][:, l * D0 : (l + 1) * D0],
+                        scalar1=1.0,
+                        scalar2=None,
+                        op0=ALU.mult,
+                        op1=ALU.add,
+                        accum_out=sx[:, a : a + 1],
+                    )
 
             def quantise_x(c):
                 nc.vector.quantize_mx(out=xq[c][:].bitcast(FP8X4), scales=xs[c][:], in_=xg[c][:])
@@ -240,6 +248,7 @@ def tile_optimalnet_pa_t_kernel(tc, x, W1, b1, W2, b2, out_0, out_1, out_2):
                     for cc in range(4):
                         sbs[cc] = spread_row_sums(cc)
                 layer1(1, c)
+                add_tiles_01(c)
                 if c == 0:
                     load_x(7)
                 if c == 2:
@@ -272,6 +281,8 @@ def tile_optimalnet_pa_t_kernel(tc, x, W1, b1, W2, b2, out_0, out_1, out_2):
         scaled_mean1(1)
         for n in range(16):
             layer1(2 + n // 8, n % 8)
+            if n < 8:
+                add_tile_2(n)
             if n % 2 == 0:
                 cc = n // 2
                 correct(0, cc, sbs[cc])
@@ -283,12 +294,14 @@ def tile_optimalnet_pa_t_kernel(tc, x, W1, b1, W2, b2, out_0, out_1, out_2):
         sb2[0] = spread_row_sums(0)
         scaled_mean1(2)
         scaled_mean1(3)
+        row_sums_v1(0, True)
+        row_sums_v1(1, True)
+        for cc in range(1, 4):
+            sb2[cc] = spread_row_sums(cc)
         kb = pz.tile([P, CW], F32, name="kb", tag="z")
         for t in range(4):
             nc.tensor.transpose(kb[:, t * P : (t + 1) * P], cm1[:, t : t + 1].to_broadcast([P, P]), ident[:])
-        nc.scalar.activation(out=ja[:], in_=kb[:], func=FN.Copy, scale=1.0 / D1, accum_out=k1[:, 0:1])
-        for cc in range(1, 4):
-            sb2[cc] = spread_row_sums(cc)
+        nc.scalar.activation(out=ja[:], in_=kb[:], func=FN.Copy, accum_out=k1[:, 0:1])
 
         hg = {}
 
@@ -302,17 +315,11 @@ def tile_optimalnet_pa_t_kernel(tc, x, W1, b1, W2, b2, out_0, out_1, out_2):
 
         hqs = {}
 
-        def v2seg(c, t, first, width):
-            return v2[c][t // 2][:, (t % 2) * CW + first : (t % 2) * CW + first + width]
-
         def quantise_h(c):
             hq = work.tile([P, CW], U32, name="hq", tag="hq", bufs=2, align_bytes=64)
             hs = work.tile([P, CW], U8, name="hs", tag="hs", bufs=2, align_bytes=64)
             nc.vector.quantize_mx(out=hq[:].bitcast(FP8X4), scales=hs[:], in_=hg[c][:])
-            v2[c] = (
-                keep.tile([P, 2 * CW], F32, name="v2lo%d" % c, tag="q%d" % c, align_bytes=64),
-                work.tile([P, 2 * CW], F32, name="v2hi%d" % c),
-            )
+            v2[c] = keep.tile([P, 4 * CW], F32, name="v2_%d" % c, tag="hv%d" % c)
             hqs[c] = (hq, hs)
 
         def layer2(c, tiles):
@@ -329,7 +336,7 @@ def tile_optimalnet_pa_t_kernel(tc, x, W1, b1, W2, b2, out_0, out_1, out_2):
                     stop=True,
                 )
                 nc.scalar.activation(
-                    out=v2seg(c, t, 0, CW),
+                    out=v2[c][:, t * CW : (t + 1) * CW],
                     in_=z[:],
                     func=FN.Relu,
                     bias=b2f[:, t : t + 1],
@@ -337,22 +344,22 @@ def tile_optimalnet_pa_t_kernel(tc, x, W1, b1, W2, b2, out_0, out_1, out_2):
                     accum_out=acc2[:, t * CH + c : t * CH + c + 1],
                 )
 
+        svbank = None
         for c in range(CH):
+            if 1 <= c <= 6:
+                svbank = row_sums_v1(c + 1, False)
             correct(2, c, sb2[c])
             correct(3, c, sb2[c])
             if c >= 1:
                 quantise_h(c - 1)
-                layer2(c - 1, (0, 1))
+            if 1 <= c <= 6:
+                reduce_row_sums(c + 1, svbank)
             if c >= 1:
-                layer2(c - 1, (2, 3))
+                layer2(c - 1, (0, 1, 2, 3))
             if c + 4 < CH:
                 sb2[c + 4] = spread_row_sums(c + 4)
             regroup(c)
             if c == 0:
-                nc.vector.tensor_scalar_mul(out=shb0[:], in0=sx[:], scalar1=k1[:, 0:1])
-                nc.vector.scalar_tensor_tensor(
-                    out=shb[:], in0=sxa[:], scalar=k1[:, 0:1], in1=shb0[:], op0=ALU.mult, op1=ALU.add
-                )
                 nc.vector.tensor_reduce(
                     out=s1[:], in_=acc1[:].rearrange("p (t c) -> p t c", t=4), axis=AXIS.X, op=ALU.add
                 )
@@ -369,19 +376,28 @@ def tile_optimalnet_pa_t_kernel(tc, x, W1, b1, W2, b2, out_0, out_1, out_2):
         quantise_h(CH - 1)
         layer2(CH - 1, (0, 1, 2, 3))
 
+        sh_v = sh[:].rearrange("p (c l) -> p c l", l=4)
+        sx_v = sx[:].rearrange("p (c l) -> p c l", l=4)
+        sv_v = sv[:].rearrange("p (c l) -> p c l", l=4)
+        nc.vector.scalar_tensor_tensor(
+            out=sh_v[:, :, 0:3], in0=sx_v[:, :, 0:3], scalar=k1[:, 0:1], in1=sv_v[:, :, 0:3], op0=ALU.mult, op1=ALU.add
+        )
+        nc.vector.scalar_tensor_tensor(
+            out=sh_v[:, :, 3], in0=sxa[:], scalar=k1[:, 0:1], in1=sv_v[:, :, 3], op0=ALU.mult, op1=ALU.add
+        )
+
         def natural(a):
-            bank = pz.tile([P, CW], F32, name="vn", tag="z")
+            bank = pt.tile([P, CW], F32, name="vn", tag="pt")
             for t in range(4):
-                nc.tensor.transpose(bank[:, t * P : (t + 1) * P], v2seg(a // 4, t, (a % 4) * P, P), ident[:])
+                first = t * CW + (a % 4) * P
+                nc.tensor.transpose(bank[:, t * P : (t + 1) * P], v2[a // 4][:, first : first + P], ident[:])
             return bank
 
         vn = {}
-        for a in range(3):
-            row_sum_h(a)
         for a in range(4):
             vn[a] = natural(a)
         nc.vector.tensor_reduce(out=s2[:], in_=acc2[:].rearrange("p (t c) -> p t c", t=4), axis=AXIS.X, op=ALU.add)
-        mb = pt.tile([P, CW], F32, name="mb", tag="pt")
+        mb = pz.tile([P, CW], F32, name="mb", tag="z")
         for t in range(4):
             nc.tensor.transpose(mb[:, t * P : (t + 1) * P], s2[:, t : t + 1].to_broadcast([P, P]), ident[:])
         nc.scalar.activation(out=cm2b[:], in_=mb[:], func=FN.Copy, scale=C / ROWS)
@@ -392,13 +408,15 @@ def tile_optimalnet_pa_t_kernel(tc, x, W1, b1, W2, b2, out_0, out_1, out_2):
         for a in range(NT):
             if a % 2 == 0:
                 ob = work.tile([P, 2 * D2], F32, name="ob", tag="ob", bufs=4)
-            half = ob[:, (a % 2) * D2 : (a % 2 + 1) * D2]
             nc.vector.scalar_tensor_tensor(
-                out=half, in0=cm2b[:], scalar=sh[:, a : a + 1], in1=vn[a][:], op0=ALU.mult, op1=ALU.add
+                out=ob[:, (a % 2) * D2 : (a % 2 + 1) * D2],
+                in0=cm2b[:],
+                scalar=sh[:, a : a + 1],
+                in1=vn[a][:],
+                op0=ALU.mult,
+                op1=ALU.add,
             )
             if a % 2 == 1:
                 nc.sync.dma_start(out=out_v[:, (a - 1) * D2 : (a + 1) * D2], in_=ob[:])
-            if a + 3 < NT:
-                row_sum_h(a + 3)
             if a + 4 < NT:
                 vn[a + 4] = natural(a + 4)

from contextlib import ExitStack

import concourse.mybir as mybir
from concourse.masks import make_identity

F32 = mybir.dt.float32
BF16 = mybir.dt.bfloat16
U32 = mybir.dt.uint32
U8 = mybir.dt.uint8
FP8X4 = mybir.dt.float8_e4m3fn_x4
ALU = mybir.AluOpType
FN = mybir.ActivationFunctionType
AXIS = mybir.AxisListType

P = 128
ROWS, D0, D1, D2 = 4096, 1024, 512, 512
C = 0.01 * 0.001 / 1
NT = ROWS // P
CH = 8
CW = 512
FLOPS = 2 * ROWS * D0 * D1 + 2 * ROWS * D1 * D2


def tile_optimalnet_pa_t_kernel(tc, x, W1, b1, W2, b2, out_0, out_1, out_2):
    nc = tc.nc
    x_v = x.rearrange("(p a) i -> p (a i)", a=NT)
    out_v = out_0.rearrange("(p a) o -> p (a o)", a=NT)

    with ExitStack() as ctx:
        ctx.enter_context(tc.manual_schedule())
        keep = ctx.enter_context(tc.tile_pool(name="keep", bufs=1))
        pt = ctx.enter_context(tc.psum_pool(name="pt", bufs=4))
        pz = ctx.enter_context(tc.psum_pool(name="pz", bufs=4))

        ht = {}
        hv = [keep.tile([P, 4 * CW], F32, name="hv%d" % c) for c in range(CH)]
        xq = [keep.tile([P, 2 * CW], U32, name="xq%d" % c, align_bytes=64) for c in range(CH)]
        sacc = [keep.tile([P, CW], F32, name="sacc%d" % c) for c in range(CH)]
        xs = [keep.tile([P, 2 * CW], U8, name="xs%d" % c, align_bytes=64) for c in range(CH)]
        w1q = keep.tile([P, 1024], U32, name="w1q", align_bytes=64)
        w1s = keep.tile([P, 1024], U8, name="w1s", align_bytes=64)
        w2q = keep.tile([P, 512], U32, name="w2q", align_bytes=64)
        w2s = keep.tile([P, 512], U8, name="w2s", align_bytes=64)
        ident = keep.tile([P, P], F32, name="ident")
        b1f = keep.tile([P, 4], F32, name="b1f")
        b2f = keep.tile([P, 4], F32, name="b2f")
        acc1 = keep.tile([P, 32], F32, name="acc1")
        acc2 = keep.tile([P, 32], F32, name="acc2")
        sx = keep.tile([P, NT], F32, name="sx")
        sxa = keep.tile([P, CH], F32, name="sxa")
        jxa = keep.tile([P, D0], BF16, name="jxa")
        sh = keep.tile([P, NT], F32, name="sh")
        sv = keep.tile([P, NT], F32, name="sv")
        k1 = keep.tile([P, 1], F32, name="k1")
        cm1 = keep.tile([P, 4], F32, name="cm1")
        s1 = keep.tile([P, 4], F32, name="s1")
        s2 = keep.tile([P, 4], F32, name="s2")
        jx = keep.tile([P, D0], BF16, name="jx")
        ja = keep.tile([P, CW], BF16, name="ja")
        j8 = keep.tile([P, 8], F32, name="j8")
        cm2b = keep.tile([P, D2], F32, name="cm2b")
        m2r = keep.tile([P, D2], F32, name="m2r")
        m1r = keep.tile([P, D1], F32, name="m1r")

        make_identity(nc, ident[:])

        def four_transposes(bank, words, first):
            for b in range(4):
                nc.tensor.transpose(
                    bank[:, b * P : (b + 1) * P], words[:, first + b * P : first + (b + 1) * P], ident[:]
                )

        def exit_words(grouped, col0, bank):
            dst = grouped[:].bitcast(F32).rearrange("q (g c u) -> q g c u", g=2, u=2)
            nc.scalar.copy(
                out=dst[:, :, col0 : col0 + P, :],
                in_=bank[:].rearrange("q (g u c) -> q g c u", g=2, u=2),
            )

        def layer1(t, c):
            z = pz.tile([P, CW], F32, name="z", tag="z")
            for g in range(2):
                wcols = slice(g * 512 + t * P, g * 512 + (t + 1) * P)
                xcols = slice(g * CW, (g + 1) * CW)
                nc.tensor.matmul_mx(
                    out=z[:],
                    lhsT=w1q[:, wcols].bitcast(FP8X4),
                    lhsT_scale=w1s[:, wcols],
                    rhs=xq[c][:, xcols].bitcast(FP8X4),
                    rhs_scale=xs[c][:, xcols],
                    start=(g == 0),
                    stop=(g == 1),
                )
            nc.scalar.activation(
                out=hv[c][:, t * CW : (t + 1) * CW],
                in_=z[:],
                func=FN.Relu,
                bias=b1f[:, t : t + 1],
                scale=1.0,
                accum_out=acc1[:, t * CH + c : t * CH + c + 1],
            )

        def add_tiles_01(c):
            nc.gpsimd.tensor_tensor(out=sacc[c][:], in0=hv[c][:, 0:CW], in1=hv[c][:, CW : 2 * CW], op=ALU.add)

        def add_tile_2(c):
            nc.gpsimd.tensor_tensor(out=sacc[c][:], in0=sacc[c][:], in1=hv[c][:, 2 * CW : 3 * CW], op=ALU.add)

        def spread_row_sums(c):
            sb = pt.tile([P, CW], F32, name="sb", tag="pt")
            for l in range(4):
                a = 4 * c + l
                col = sxa[:, c : c + 1] if l == 3 else sx[:, a : a + 1]
                nc.tensor.transpose(sb[:, l * P : (l + 1) * P], col.to_broadcast([P, P]), ident[:])
            return sb

        def scaled_mean1(t):
            nc.vector.tensor_scalar(
                out=j8[:],
                in0=acc1[:, t * CH : (t + 1) * CH],
                scalar1=C / ROWS,
                scalar2=None,
                op0=ALU.mult,
                op1=ALU.add,
                accum_out=cm1[:, t : t + 1],
            )

        def correct(t, c, sb):
            seg = slice(t * CW, (t + 1) * CW)
            nc.vector.scalar_tensor_tensor(
                out=ht[c][:, seg], in0=sb[:], scalar=cm1[:, t : t + 1], in1=hv[c][:, seg], op0=ALU.mult, op1=ALU.add
            )

        def row_sums_v1(c, on_scalar):
            bank = pz.tile([P, CW], F32, name="svb", tag="z")
            for l in range(4):
                parts = (sacc[c][:, l * P : (l + 1) * P], hv[c][:, 3 * CW + l * P : 3 * CW + (l + 1) * P])
                for k in range(2):
                    nc.tensor.matmul(
                        out=bank[:, l * P : (l + 1) * P],
                        lhsT=parts[k],
                        rhs=ident[:],
                        is_transpose=True,
                        start=(k == 0),
                        stop=(k == 1),
                    )
            if on_scalar:
                for l in range(4):
                    a = 4 * c + l
                    nc.scalar.activation(
                        out=ja[:, 0:P], in_=bank[:, l * P : (l + 1) * P], func=FN.Copy, accum_out=sv[:, a : a + 1]
                    )
            return bank

        def reduce_row_sums(c, bank):
            nc.vector.tensor_reduce(
                out=sv[:, 4 * c : 4 * c + 4], in_=bank[:].rearrange("p (l k) -> p l k", l=4), axis=AXIS.X, op=ALU.add
            )

        with tc.tile_pool(name="stage", bufs=1) as stage:
            xn = {}

            def load_x(c):
                xt = stage.tile([P, 4 * D0], BF16, name="xn", tag="xn", bufs=5)
                nc.sync.dma_start(out=xt[:], in_=x_v[:, c * 4 * D0 : (c + 1) * 4 * D0])
                xn[c] = xt

            xg = {}

            def transpose_x(c):
                g_t = stage.tile([P, 4 * D0], BF16, name="xg", tag="xg", bufs=2, align_bytes=64)
                xg[c] = g_t
                words = xn[c][:].bitcast(F32)
                for l in range(4):
                    bank = pt.tile([P, CW], F32, name="xt", tag="pt")
                    four_transposes(bank, words, l * 512)
                    exit_words(g_t, l * P, bank)

            def row_sums_x(c):
                nc.scalar.activation(
                    out=jxa[:], in_=xn[c][:, 3 * D0 : 4 * D0], func=FN.Copy, accum_out=sxa[:, c : c + 1]
                )
                for l in range(3):
                    a = 4 * c + l
                    nc.vector.tensor_scalar(
                        out=jx[:],
                        in0=xn[c][:, l * D0 : (l + 1) * D0],
                        scalar1=1.0,
                        scalar2=None,
                        op0=ALU.mult,
                        op1=ALU.add,
                        accum_out=sx[:, a : a + 1],
                    )

            def quantise_x(c):
                nc.vector.quantize_mx(out=xq[c][:].bitcast(FP8X4), scales=xs[c][:], in_=xg[c][:])

            w1n = stage.tile([P, 4 * D0], BF16, name="w1n")
            w1g = stage.tile([P, 4 * D0], BF16, name="w1g", align_bytes=64)
            w2n = stage.tile([P, 4 * D1], BF16, name="w2n")
            w2g = stage.tile([P, 4 * D1], BF16, name="w2g", align_bytes=64)
            b1r = stage.tile([P, 4], BF16, name="b1r")
            b2r = stage.tile([4, P], BF16, name="b2r")
            b2pad = stage.tile([P, P], F32, name="b2pad")

            first = stage.tile([P, 4 * D0], BF16, name="xn", tag="xn", bufs=5)
            xn[0] = first
            for l in range(4):
                nc.sync.dma_start(out=first[:, l * D0 : (l + 1) * D0], in_=x_v[:, l * D0 : (l + 1) * D0])
            nc.sync.dma_start(out=w1n[:], in_=W1.rearrange("(p t) i -> p (t i)", t=4))
            load_x(1)
            nc.sync.dma_start(
                out=w2n[:].rearrange("p (t o) -> p t o", t=4), in_=W2.rearrange("(t p) o -> p t o", p=P)
            )
            for c in range(2, 5):
                load_x(c)
            nc.scalar.dma_start(out=b1r[:], in_=b1.rearrange("(p t) -> p t", t=4))
            nc.scalar.dma_start(out=b2r[:], in_=b2.rearrange("(t p) -> t p", p=P))

            nc.vector.memset(b2pad[:], 0.0)
            nc.vector.tensor_copy(out=b1f[:], in_=b1r[:])
            nc.vector.tensor_copy(out=b2pad[0:4, :], in_=b2r[:])

            transpose_x(0)
            row_sums_x(0)
            w1words = w1n[:].bitcast(F32)
            for t in range(4):
                bank = pt.tile([P, CW], F32, name="w1t", tag="pt")
                four_transposes(bank, w1words, t * 512)
                exit_words(w1g, t * P, bank)
            nc.vector.quantize_mx(out=w1q[:].bitcast(FP8X4), scales=w1s[:], in_=w1g[:])
            transpose_x(1)
            row_sums_x(1)
            load_x(5)
            load_x(6)

            sbs = {}
            for c in range(CH):
                quantise_x(c)
                if c + 2 < CH - 2:
                    row_sums_x(c + 2)
                if c >= CH - 2:
                    row_sums_x(c)
                layer1(0, c)
                if c + 2 < CH:
                    transpose_x(c + 2)
                if c == CH - 1:
                    for cc in range(4):
                        sbs[cc] = spread_row_sums(cc)
                layer1(1, c)
                add_tiles_01(c)
                if c == 0:
                    load_x(7)
                if c == 2:
                    w2words = w2n[:].bitcast(F32).rearrange("p (t w u) -> p t u w", t=4, u=2)
                    w2gw = w2g[:].bitcast(F32).rearrange("q (t c u) -> q t c u", t=4, u=2)
                    for h in range(2):
                        bank = pt.tile([P, CW], F32, name="w2t", tag="pt")
                        for tl in range(2):
                            for u in range(2):
                                k = tl * 2 + u
                                nc.tensor.transpose(
                                    bank[:, k * P : (k + 1) * P], w2words[:, 2 * h + tl, u, :], ident[:]
                                )
                        nc.scalar.copy(
                            out=w2gw[:, 2 * h : 2 * h + 2, :, :],
                            in_=bank[:].rearrange("q (t u c) -> q t c u", t=2, u=2),
                        )
                    bank = pt.tile([P, CW], F32, name="b2t", tag="pt")
                    nc.tensor.transpose(bank[:, 0:P], b2pad[:], ident[:])
                    nc.scalar.copy(out=b2f[:], in_=bank[:, 0:4])
                if c == 3:
                    nc.vector.quantize_mx(out=w2q[:].bitcast(FP8X4), scales=w2s[:], in_=w2g[:])

        work = ctx.enter_context(tc.tile_pool(name="work", bufs=1))
        for c in range(CH):
            ht[c] = work.tile([P, 4 * CW], BF16, name="ht%d" % c)
        v2 = {}

        scaled_mean1(0)
        scaled_mean1(1)
        for n in range(16):
            layer1(2 + n // 8, n % 8)
            if n < 8:
                add_tile_2(n)
            if n % 2 == 0:
                cc = n // 2
                correct(0, cc, sbs[cc])
                correct(1, cc, sbs[cc])
            if n in (6, 8, 10, 12):
                cc = 4 + (n - 6) // 2
                sbs[cc] = spread_row_sums(cc)
        sb2 = {}
        sb2[0] = spread_row_sums(0)
        scaled_mean1(2)
        scaled_mean1(3)
        row_sums_v1(0, True)
        row_sums_v1(1, True)
        for cc in range(1, 4):
            sb2[cc] = spread_row_sums(cc)
        kb = pz.tile([P, CW], F32, name="kb", tag="z")
        for t in range(4):
            nc.tensor.transpose(kb[:, t * P : (t + 1) * P], cm1[:, t : t + 1].to_broadcast([P, P]), ident[:])
        nc.scalar.activation(out=ja[:], in_=kb[:], func=FN.Copy, accum_out=k1[:, 0:1])

        hg = {}

        def regroup(c):
            g_t = work.tile([P, 4 * CW], BF16, name="hg", tag="hg", bufs=2, align_bytes=64)
            hg[c] = g_t
            nc.vector.tensor_copy(
                out=g_t[:].rearrange("p (c i t) -> p c t i", i=4, t=4),
                in_=ht[c][:].rearrange("p (t c i) -> p c t i", t=4, i=4),
            )

        hqs = {}

        def quantise_h(c):
            hq = work.tile([P, CW], U32, name="hq", tag="hq", bufs=2, align_bytes=64)
            hs = work.tile([P, CW], U8, name="hs", tag="hs", bufs=2, align_bytes=64)
            nc.vector.quantize_mx(out=hq[:].bitcast(FP8X4), scales=hs[:], in_=hg[c][:])
            v2[c] = keep.tile([P, 4 * CW], F32, name="v2_%d" % c, tag="hv%d" % c)
            hqs[c] = (hq, hs)

        def layer2(c, tiles):
            hq, hs = hqs[c]
            for t in tiles:
                z = pz.tile([P, CW], F32, name="z2", tag="z")
                nc.tensor.matmul_mx(
                    out=z[:],
                    lhsT=w2q[:, t * P : (t + 1) * P].bitcast(FP8X4),
                    lhsT_scale=w2s[:, t * P : (t + 1) * P],
                    rhs=hq[:].bitcast(FP8X4),
                    rhs_scale=hs[:],
                    start=True,
                    stop=True,
                )
                nc.scalar.activation(
                    out=v2[c][:, t * CW : (t + 1) * CW],
                    in_=z[:],
                    func=FN.Relu,
                    bias=b2f[:, t : t + 1],
                    scale=1.0,
                    accum_out=acc2[:, t * CH + c : t * CH + c + 1],
                )

        svbank = None
        for c in range(CH):
            if 1 <= c <= 6:
                svbank = row_sums_v1(c + 1, False)
            correct(2, c, sb2[c])
            correct(3, c, sb2[c])
            if c >= 1:
                quantise_h(c - 1)
            if 1 <= c <= 6:
                reduce_row_sums(c + 1, svbank)
            if c >= 1:
                layer2(c - 1, (0, 1, 2, 3))
            if c + 4 < CH:
                sb2[c + 4] = spread_row_sums(c + 4)
            regroup(c)
            if c == 0:
                nc.vector.tensor_reduce(
                    out=s1[:], in_=acc1[:].rearrange("p (t c) -> p t c", t=4), axis=AXIS.X, op=ALU.add
                )
                m1b = pz.tile([P, CW], F32, name="m1b", tag="z")
                for t in range(4):
                    nc.tensor.transpose(m1b[:, t * P : (t + 1) * P], s1[:, t : t + 1].to_broadcast([P, P]), ident[:])
                nc.scalar.activation(
                    out=m1r[0:32, :].rearrange("p (k t) -> p k t", t=4),
                    in_=m1b[0:32, :].rearrange("p (t k) -> p k t", t=4),
                    func=FN.Copy,
                    scale=1.0 / ROWS,
                )
                nc.sync.dma_start(out=out_1.rearrange("(o n) -> o n", o=1), in_=m1r[0:1, :])
        quantise_h(CH - 1)
        layer2(CH - 1, (0, 1, 2, 3))

        sh_v = sh[:].rearrange("p (c l) -> p c l", l=4)
        sx_v = sx[:].rearrange("p (c l) -> p c l", l=4)
        sv_v = sv[:].rearrange("p (c l) -> p c l", l=4)
        nc.vector.scalar_tensor_tensor(
            out=sh_v[:, :, 0:3], in0=sx_v[:, :, 0:3], scalar=k1[:, 0:1], in1=sv_v[:, :, 0:3], op0=ALU.mult, op1=ALU.add
        )
        nc.vector.scalar_tensor_tensor(
            out=sh_v[:, :, 3], in0=sxa[:], scalar=k1[:, 0:1], in1=sv_v[:, :, 3], op0=ALU.mult, op1=ALU.add
        )

        def natural(a):
            bank = pt.tile([P, CW], F32, name="vn", tag="pt")
            for t in range(4):
                first = t * CW + (a % 4) * P
                nc.tensor.transpose(bank[:, t * P : (t + 1) * P], v2[a // 4][:, first : first + P], ident[:])
            return bank

        vn = {}
        for a in range(4):
            vn[a] = natural(a)
        nc.vector.tensor_reduce(out=s2[:], in_=acc2[:].rearrange("p (t c) -> p t c", t=4), axis=AXIS.X, op=ALU.add)
        mb = pz.tile([P, CW], F32, name="mb", tag="z")
        for t in range(4):
            nc.tensor.transpose(mb[:, t * P : (t + 1) * P], s2[:, t : t + 1].to_broadcast([P, P]), ident[:])
        nc.scalar.activation(out=cm2b[:], in_=mb[:], func=FN.Copy, scale=C / ROWS)
        nc.scalar.activation(out=m2r[0:32, :], in_=mb[0:32, :], func=FN.Copy, scale=1.0 / ROWS)
        nc.sync.dma_start(out=out_2.rearrange("(o n) -> o n", o=1), in_=m2r[0:1, :])

        ob = None
        for a in range(NT):
            if a % 2 == 0:
                ob = work.tile([P, 2 * D2], F32, name="ob", tag="ob", bufs=4)
            nc.vector.scalar_tensor_tensor(
                out=ob[:, (a % 2) * D2 : (a % 2 + 1) * D2],
                in0=cm2b[:],
                scalar=sh[:, a : a + 1],
                in1=vn[a][:],
                op0=ALU.mult,
                op1=ALU.add,
            )
            if a % 2 == 1:
                nc.sync.dma_start(out=out_v[:, (a - 1) * D2 : (a + 1) * D2], in_=ob[:])
            if a + 4 < NT:
                vn[a + 4] = natural(a + 4)
